import numpy as np
import ml_dtypes


def mxq(x, axis, fmt="e4m3"):
    dtype, down = {"e4m3": (ml_dtypes.float8_e4m3fn, 7), "e5m2": (ml_dtypes.float8_e5m2, 14)}[fmt]
    v = np.moveaxis(np.asarray(x, np.float32).astype(ml_dtypes.bfloat16).astype(np.float64), axis, -1)
    blocks = v.reshape(v.shape[:-1] + (-1, 32))
    amax = np.abs(blocks).max(-1, keepdims=True)
    byte = np.maximum(np.where(amax > 0, np.frexp(amax)[1] - 1 + 127, 0) - down, 1)
    scale = np.exp2(byte - 127.0)
    codes = (blocks / scale).astype(np.float32).astype(dtype).astype(np.float64)
    return np.moveaxis((codes * scale).reshape(v.shape), -1, axis)


WIDE = False


def mx_kscale(k):
    if not WIDE:
        return np.ones(k)
    levels = np.array([10, -10, 5, -5, 0])
    if k % 512:
        return np.exp2(np.random.permutation(np.resize(levels, k // 32))).repeat(32)
    a = np.empty((k // 512, 16))
    for p in range(k // 512):
        a[p, :8] = np.random.permutation(np.resize(levels, 8))
        for g in range(8):
            far = levels[np.abs(levels - a[p, g]) >= 10]
            a[p, g + 8] = far[np.random.randint(len(far))]
    return np.exp2(a.ravel()).repeat(32)


BF16 = ml_dtypes.bfloat16


def bf(x):
    return np.asarray(x, np.float32).astype(BF16)


def f64(x):
    return np.asarray(x).astype(np.float64)


N, D, K = 2048, 512, 2048
S = 5.0


def rbf_values(data, centers):
    x2 = np.sum(data * data, axis=-1, keepdims=True)
    c2 = np.sum(centers * centers, axis=-1)[None, :]
    return np.exp(-S * (x2 + c2 - 2.0 * (data @ centers.T)))


def setup_inputs():
    s = mx_kscale(N)[:, None]
    u = mx_kscale(K)
    m = np.random.standard_normal(D) / np.sqrt(D)
    data0 = bf(m + np.random.standard_normal((N, D)) * 0.4 / np.sqrt(D))
    centers0 = bf(m + np.random.standard_normal((K, D)) * 0.4 / np.sqrt(D))
    rbfs = rbf_values(f64(data0), f64(centers0))
    g = 4.0 * np.random.standard_normal((N, 1 + D + K)) * np.exp2(np.random.randint(-6, 1, (N, 1)))
    g = g / s
    g = np.concatenate([g[:, :1 + D], g[:, 1 + D:] * u], axis=1)
    return {"data": bf(f64(data0) * s), "centers": bf(f64(centers0) / u[:, None]),
            "rbfs": np.asarray(rbfs, np.float32), "grad_out": bf(g)}


def reference(data, centers, rbfs, grad_out):
    data, centers, rbfs, g = f64(data), f64(centers), f64(rbfs), f64(grad_out)
    g_data = g[:, 1:1 + D]
    dz = 2.0 * S * g[:, 1 + D:] * rbfs
    row = np.sum(dz, axis=1, keepdims=True)
    col = np.sum(dz, axis=0)[:, None]
    p = mxq(dz, 1, "e5m2") @ mxq(centers, 0, "e4m3")
    q = mxq(dz, 0, "e5m2").T @ mxq(data, 0, "e4m3")
    ddata = p - data * row + g_data
    dcenters = q - centers * col
    return ddata, dcenters

@@ -1,0 +1,279 @@
+from contextlib import ExitStack
+
+import concourse.mybir as mybir
+from concourse.masks import make_identity
+
+N, D, K = 2048, 512, 2048
+FLOPS = 2 * 2 * N * K * D
+
+F32 = mybir.dt.float32
+BF16 = mybir.dt.bfloat16
+U32 = mybir.dt.uint32
+U8 = mybir.dt.uint8
+E4 = mybir.dt.float8_e4m3fn_x4
+E5 = mybir.dt.float8_e5m2_x4
+MULT = mybir.AluOpType.mult
+ADD = mybir.AluOpType.add
+SUB = mybir.AluOpType.subtract
+AX = mybir.AxisListType.X
+
+P = 128
+J = 4
+KP = P * J
+W = 1024
+NG = N // KP
+NH = K // W
+NC = W // KP
+UNITS = NG * NH
+
+
+def tile_dicgaussianrbf_v_kernel(tc, data, centers, rbfs, grad_out, out_0, out_1):
+    nc = tc.nc
+    with ExitStack() as ctx:
+        keep = ctx.enter_context(tc.tile_pool(name="keep", bufs=1))
+        ldp = ctx.enter_context(tc.tile_pool(name="ld", bufs=3))
+        dzp = ctx.enter_context(tc.tile_pool(name="dz", bufs=2))
+        mid = ctx.enter_context(tc.tile_pool(name="mid", bufs=2))
+        cod = ctx.enter_context(tc.tile_pool(name="cod", bufs=1))
+        outp = ctx.enter_context(tc.tile_pool(name="outp", bufs=4))
+        psz = ctx.enter_context(tc.psum_pool(name="psz", bufs=3))
+        psc = ctx.enter_context(tc.psum_pool(name="psc", bufs=2))
+        psm = ctx.enter_context(tc.psum_pool(name="psm", bufs=3))
+
+        ident = keep.tile([P, P], F32, name="ident")
+        make_identity(nc, ident[:])
+        warm = keep.tile([P, 1], F32, name="warm")
+        nc.vector.memset(warm[:], 0.0)
+        nc.scalar.copy(warm[:], ident[:, 0:1])
+
+        data_sb = keep.tile([P, NG, J, D], BF16, name="data_sb", align_bytes=64)
+        cent_sb = keep.tile([P, NG, J, D], BF16, name="cent_sb", align_bytes=64)
+        data_q = keep.tile([P, NG, D], U32, name="data_q", align_bytes=64)
+        data_s = keep.tile([P, NG, D], U8, name="data_s", align_bytes=64)
+        cent_q = keep.tile([P, NG, D], U32, name="cent_q", align_bytes=64)
+        cent_s = keep.tile([P, NG, D], U8, name="cent_s", align_bytes=64)
+        rowp = keep.tile([P, NG, NH, J], F32, name="rowp")
+        nrow = keep.tile([P, NG, J], F32, name="nrow")
+        colp = keep.tile([P, NH, NC, NG, J], F32, name="colp")
+        ncol = keep.tile([P, NH, NC, J], F32, name="ncol")
+
+        g_t, r_t, dz_t, x_t, z_t = {}, {}, {}, {}, {}
+        xq, xs, zq, zs, gd_t = {}, {}, {}, {}, {}
+        col_b, mm0, mm1, ost = {}, {}, {}, {}
+
+        def gh(s):
+            return s % NG, s // NG
+
+        def load_unit(s, jp):
+            g, h = gh(s)
+            gt = ldp.tile([P, 2, W], BF16, name="gt", tag="gt", bufs=3, align_bytes=64)
+            rt = ldp.tile([P, 2, W], F32, name="rt", tag="rt", bufs=3, align_bytes=64)
+            rows = slice(g * KP, (g + 1) * KP)
+            gv = grad_out[rows, 1 + D + h * W : 1 + D + (h + 1) * W].rearrange("(p j) w -> p j w", j=J)
+            rv = rbfs[rows, h * W : (h + 1) * W].rearrange("(p j) w -> p j w", j=J)
+            nc.sync.dma_start(out=gt[:], in_=gv[:, 2 * jp : 2 * jp + 2, :])
+            nc.sync.dma_start(out=rt[:], in_=rv[:, 2 * jp : 2 * jp + 2, :])
+            g_t[s, jp], r_t[s, jp] = gt, rt
+
+        def load_dc(dst, src, g):
+            nc.sync.dma_start(out=dst[:, g, :, :], in_=src[g * KP : (g + 1) * KP, :].rearrange("(p j) w -> p j w", j=J))
+
+        def load_gd(g):
+            t = ldp.tile([P, J, D], BF16, name="gd", tag="gd", bufs=2, align_bytes=64)
+            nc.sync.dma_start(out=t[:], in_=grad_out[g * KP : (g + 1) * KP, 1 : 1 + D].rearrange("(p j) w -> p j w", j=J))
+            gd_t[g] = t
+
+        def stt(s, j):
+            g, h = gh(s)
+            if j == 0:
+                dz_t[s] = dzp.tile([P, J, W], F32, name="dzt", tag="dzt", bufs=2, align_bytes=64)
+            nc.vector.scalar_tensor_tensor(
+                out=dz_t[s][:, j, :].rearrange("p (t q) -> p q t", t=J),
+                in0=g_t[s, j // 2][:, j % 2, :].rearrange("p (q t) -> p q t", t=J),
+                scalar=10.0,
+                in1=r_t[s, j // 2][:, j % 2, :].rearrange("p (q t) -> p q t", t=J),
+                op0=MULT, op1=MULT,
+                accum_out=rowp[:, g, h, j : j + 1],
+            )
+
+        def transp(s, j):
+            for c in range(NC):
+                b = psz.tile([P, J, P], F32, name="zb", tag="zb", bufs=3)
+                for t in range(J):
+                    a = t * (W // J) + c * P
+                    nc.tensor.transpose(b[:, t, :], dz_t[s][:, j, a : a + P], ident[:])
+                if (s, c) not in z_t:
+                    z_t[s, c] = mid.tile([P, J, P, J], BF16, name="zt", tag="zt", bufs=3, align_bytes=64)
+                nc.scalar.copy(z_t[s, c][:, j, :, :], b[:].rearrange("p t r -> p r t"))
+
+        def xpiece(s, k):
+            if k % 2 == 0:
+                x_t[s, k // 2] = mid.tile([P, W // 2, J], BF16, name="xt", tag="xt", bufs=2, align_bytes=64)
+            w = W // 4
+            nc.scalar.copy(
+                x_t[s, k // 2][:, (k % 2) * w : (k % 2 + 1) * w, :].rearrange("p (c i) j -> p c j i", i=4),
+                dz_t[s][:, :, k * w : (k + 1) * w].rearrange("p j (c i) -> p c j i", i=4),
+            )
+
+        def qz(s, c):
+            if c == 0:
+                zq[s] = cod.tile([P, NC, KP], U32, name="zqt", tag="zqt", bufs=6, align_bytes=64)
+                zs[s] = cod.tile([P, NC, KP], U8, name="zst", tag="zst", bufs=6, align_bytes=64)
+            nc.vector.quantize_mx(out=zq[s][:, c, :].bitcast(E5), scales=zs[s][:, c, :],
+                                  in_=z_t[s, c][:].rearrange("p j r t -> p (j r t)"))
+
+        def qx(s, k):
+            if k == 0:
+                xq[s] = cod.tile([P, W], U32, name="xqt", tag="xqt", bufs=5, align_bytes=64)
+                xs[s] = cod.tile([P, W], U8, name="xst", tag="xst", bufs=5, align_bytes=64)
+            sl = slice(k * W // 2, (k + 1) * W // 2)
+            nc.vector.quantize_mx(out=xq[s][:, sl].bitcast(E5), scales=xs[s][:, sl],
+                                  in_=x_t[s, k][:].rearrange("p w j -> p (w j)"))
+
+        dc_t = {}
+
+        def dc_copy(name, src, g, eng):
+            t = mid.tile([P, D, J], BF16, name="dct", tag="dct", bufs=2, align_bytes=64)
+            o = t[:].rearrange("p (c i) j -> p c j i", i=4)
+            i_ = src[:, g, :, :].rearrange("p j (c i) -> p c j i", i=4)
+            if eng == 0:
+                nc.vector.tensor_copy(o, i_)
+            else:
+                nc.scalar.copy(o, i_)
+            dc_t[name, g] = t
+
+        def dc_quant(name, q, sc, g):
+            nc.vector.quantize_mx(out=q[:, g, :].bitcast(E4), scales=sc[:, g, :],
+                                  in_=dc_t[name, g][:].rearrange("p w j -> p (w j)"))
+
+        def col_t(s):
+            for c in range(NC):
+                b = psc.tile([P, J, P], F32, name="cb", tag="cb", bufs=2)
+                for t in range(J):
+                    a = t * (W // J) + c * P
+                    for j in range(J):
+                        nc.tensor.matmul(b[:, t, :], lhsT=dz_t[s][:, j, a : a + P], rhs=ident[:],
+                                         is_transpose=True, start=(j == 0), stop=(j == J - 1))
+                col_b[s, c] = b
+
+        def col_r(s):
+            g, h = gh(s)
+            for c in range(NC):
+                nc.vector.tensor_reduce(colp[:, h, c, g, :], col_b[s, c][:], AX, ADD)
+
+        def nrow_f(g):
+            nc.vector.scalar_tensor_tensor(out=nrow[:, g, :], in0=rowp[:, g, 0, :], scalar=-1.0, in1=rowp[:, g, 1, :],
+                                           op0=MULT, op1=SUB)
+
+        def ncol_f(h):
+            tmp = keep.tile([P, NC, J], F32, name="ctmp", tag="ctmp", bufs=1)
+            nc.vector.tensor_reduce(tmp[:], colp[:, h, :, :, :].rearrange("p c g t -> p c t g"), AX, ADD)
+            nc.vector.tensor_scalar(ncol[:, h, :, :], tmp[:], -1.0, None, op0=MULT)
+
+        def mx0(g, j):
+            b = psm.tile([P, D], F32, name="mb", tag="mb", bufs=3)
+            for cc in range(NH * NC):
+                s = (cc // NC) * NG + g
+                nc.tensor.matmul_mx(
+                    out=b[:],
+                    lhsT=zq[s][:, cc % NC, j * P : (j + 1) * P].bitcast(E5),
+                    lhsT_scale=zs[s][:, cc % NC, j * P : (j + 1) * P],
+                    rhs=cent_q[:, cc, :].bitcast(E4), rhs_scale=cent_s[:, cc, :],
+                    start=(cc == 0), stop=(cc == NH * NC - 1))
+            mm0[g, j] = b
+
+        def mx1(h, c, t):
+            b = psm.tile([P, D], F32, name="mb", tag="mb", bufs=3)
+            a = t * (W // J) + c * P
+            for g in range(NG):
+                s = h * NG + g
+                nc.tensor.matmul_mx(
+                    out=b[:],
+                    lhsT=xq[s][:, a : a + P].bitcast(E5), lhsT_scale=xs[s][:, a : a + P],
+                    rhs=data_q[:, g, :].bitcast(E4), rhs_scale=data_s[:, g, :],
+                    start=(g == 0), stop=(g == NG - 1))
+            mm1[h, c, t] = b
+
+        def epi0a(g, j):
+            if j % 2 == 0:
+                ost[0, g, j // 2] = outp.tile([P, 2, D], F32, name="o", tag="o", bufs=4, align_bytes=64)
+            o = ost[0, g, j // 2]
+            nc.vector.scalar_tensor_tensor(out=o[:, j % 2, :], in0=data_sb[:, g, j, :], scalar=nrow[:, g, j : j + 1],
+                                           in1=mm0[g, j][:], op0=MULT, op1=ADD)
+
+        def epi0b(g, jp):
+            o = ost[0, g, jp]
+            nc.vector.tensor_tensor(out=o[:], in0=o[:], in1=gd_t[g][:, 2 * jp : 2 * jp + 2, :], op=ADD)
+            nc.sync.dma_start(out=out_0[g * KP : (g + 1) * KP, :].rearrange("(p j) w -> p j w", j=J)[:, 2 * jp : 2 * jp + 2, :],
+                              in_=o[:])
+
+        def epi1(h, c, t):
+            if t % 2 == 0:
+                ost[1, h, c, t // 2] = outp.tile([P, 2, D], F32, name="o", tag="o", bufs=4, align_bytes=64)
+            o = ost[1, h, c, t // 2]
+            cc = h * NC + c
+            nc.vector.scalar_tensor_tensor(out=o[:, t % 2, :], in0=cent_sb[:, cc, t, :], scalar=ncol[:, h, c, t : t + 1],
+                                           in1=mm1[h, c, t][:], op0=MULT, op1=ADD)
+            if t % 2 == 1:
+                tp = t // 2
+                nc.sync.dma_start(out=out_1[cc * KP : (cc + 1) * KP, :].rearrange("(p j) w -> p j w", j=J)[:, 2 * tp : 2 * tp + 2, :],
+                                  in_=o[:])
+
+        for s in range(UNITS + 1):
+            g, h = gh(s)
+            if s < UNITS:
+                load_unit(s, 0)
+                load_unit(s, 1)
+            if s < NG:
+                load_dc(data_sb, data, g)
+                load_dc(cent_sb, centers, g)
+            elif s < UNITS:
+                load_gd(g)
+            for j in range(J):
+                if s < UNITS:
+                    stt(s, j)
+                    if s >= 1:
+                        xpiece(s - 1, j)
+                    if j == 0 and s >= 1:
+                        col_t(s - 1)
+                    transp(s, j)
+                else:
+                    xpiece(s - 1, j)
+                    if j == 0:
+                        col_t(s - 1)
+                if s >= 1:
+                    if j < 2:
+                        qz(s - 1, j)
+                    if j == 2:
+                        col_r(s - 1)
+                        qx(s - 1, 0)
+                    if j == 3:
+                        qx(s - 1, 1)
+                if s < NG:
+                    if j == 1:
+                        dc_copy("d", data_sb, g, 0)
+                    if j == 2:
+                        dc_copy("c", cent_sb, g, 1)
+                        dc_quant("d", data_q, data_s, g)
+                    if j == 3:
+                        dc_quant("c", cent_q, cent_s, g)
+            if s > NG:
+                gp = (s - 1) % NG
+                nrow_f(gp)
+                for j in range(J):
+                    mx0(gp, j)
+                    epi0a(gp, j)
+                    if j % 2 == 1:
+                        epi0b(gp, j // 2)
+            if s == NG:
+                ncol_f(0)
+            if s == NG + 1 or s == NG + 2:
+                for t in range(J):
+                    mx1(0, s - NG - 1, t)
+                    epi1(0, s - NG - 1, t)
+            if s == UNITS:
+                ncol_f(1)
+                for c in range(NC):
+                    for t in range(J):
+                        mx1(1, c, t)
+                        epi1(1, c, t)

@@ -20,25 +20,22 @@ AX = mybir.AxisListType.X
 P = 128
 J = 4
 KP = P * J
-W = 1024
 NG = N // KP
-NH = K // W
-NC = W // KP
-UNITS = NG * NH
+NCC = K // KP
+UNITS = [(0, 2, 2), (0, 0, 2), (1, 0, 2), (2, 0, 2), (3, 0, 2), (1, 2, 2), (2, 2, 2), (3, 2, 1), (3, 3, 1)]
+NU = len(UNITS)
+XQB = {"xa": 4, "xb": 3}
+RS = (3, 4, 5)
+GROUPS = [(0,), (1, 2), (3, 4), (5, 6), (7,), (8,)]
+XV = ()
 
 
 def tile_dicgaussianrbf_v_kernel(tc, data, centers, rbfs, grad_out, out_0, out_1):
     nc = tc.nc
     with ExitStack() as ctx:
         keep = ctx.enter_context(tc.tile_pool(name="keep", bufs=1))
-        ldp = ctx.enter_context(tc.tile_pool(name="ld", bufs=3))
-        dzp = ctx.enter_context(tc.tile_pool(name="dz", bufs=2))
-        mid = ctx.enter_context(tc.tile_pool(name="mid", bufs=2))
-        cod = ctx.enter_context(tc.tile_pool(name="cod", bufs=1))
-        outp = ctx.enter_context(tc.tile_pool(name="outp", bufs=4))
-        psz = ctx.enter_context(tc.psum_pool(name="psz", bufs=3))
-        psc = ctx.enter_context(tc.psum_pool(name="psc", bufs=2))
-        psm = ctx.enter_context(tc.psum_pool(name="psm", bufs=3))
+        sb = ctx.enter_context(tc.tile_pool(name="sb", bufs=1))
+        ps = ctx.enter_context(tc.psum_pool(name="ps", bufs=1))
 
         ident = keep.tile([P, P], F32, name="ident")
         make_identity(nc, ident[:])
@@ -52,88 +49,124 @@ def tile_dicgaussianrbf_v_kernel(tc, data, centers, rbfs, grad_out, out_0, out_1
         data_s = keep.tile([P, NG, D], U8, name="data_s", align_bytes=64)
         cent_q = keep.tile([P, NG, D], U32, name="cent_q", align_bytes=64)
         cent_s = keep.tile([P, NG, D], U8, name="cent_s", align_bytes=64)
-        rowp = keep.tile([P, NG, NH, J], F32, name="rowp")
+        rowp = keep.tile([P, NG, NCC, J], F32, name="rowp")
         nrow = keep.tile([P, NG, J], F32, name="nrow")
-        colp = keep.tile([P, NH, NC, NG, J], F32, name="colp")
-        ncol = keep.tile([P, NH, NC, J], F32, name="ncol")
+        colp = keep.tile([P, NCC, J, 3], F32, name="colp")
+        ncol = keep.tile([P, NCC, J], F32, name="ncol")
+        nc.vector.memset(colp[:], 0.0)
 
         g_t, r_t, dz_t, x_t, z_t = {}, {}, {}, {}, {}
-        xq, xs, zq, zs, gd_t = {}, {}, {}, {}, {}
-        col_b, mm0, mm1, ost = {}, {}, {}, {}
+        zloc, xloc, gd_t, col_b, dc_t, ost, ncolg = {}, {}, {}, {}, {}, {}, {}
 
-        def gh(s):
-            return s % NG, s // NG
+        def bank(tag, bufs):
+            return ps.tile([P, J, P], F32, name=tag, tag=tag, bufs=bufs)
 
-        def load_unit(s, jp):
-            g, h = gh(s)
-            gt = ldp.tile([P, 2, W], BF16, name="gt", tag="gt", bufs=3, align_bytes=64)
-            rt = ldp.tile([P, 2, W], F32, name="rt", tag="rt", bufs=3, align_bytes=64)
+        def load_j(n):
+            u, j = n // J, n % J
+            if u >= NU:
+                return
+            g, c0, ncs = UNITS[u]
+            w = ncs * KP
             rows = slice(g * KP, (g + 1) * KP)
-            gv = grad_out[rows, 1 + D + h * W : 1 + D + (h + 1) * W].rearrange("(p j) w -> p j w", j=J)
-            rv = rbfs[rows, h * W : (h + 1) * W].rearrange("(p j) w -> p j w", j=J)
-            nc.sync.dma_start(out=gt[:], in_=gv[:, 2 * jp : 2 * jp + 2, :])
-            nc.sync.dma_start(out=rt[:], in_=rv[:, 2 * jp : 2 * jp + 2, :])
-            g_t[s, jp], r_t[s, jp] = gt, rt
+            if j % 2 == 0:
+                gt = sb.tile([P, 2, w], BF16, name="gt", tag="gt", bufs=3, align_bytes=64)
+                g_t[u, j // 2] = gt
+                gv = grad_out[rows, 1 + D + c0 * KP : 1 + D + c0 * KP + w].rearrange("(p j) w -> p j w", j=J)
+                if n == 0:
+                    nc.sync.dma_start(out=gt[:, 0, :], in_=gv[:, 0, :])
+                else:
+                    nc.sync.dma_start(out=gt[:], in_=gv[:, j : j + 2, :])
+            elif n == 1:
+                gv = grad_out[rows, 1 + D + c0 * KP : 1 + D + c0 * KP + w].rearrange("(p j) w -> p j w", j=J)
+                nc.sync.dma_start(out=g_t[u, 0][:, 1, :], in_=gv[:, 1, :])
+            rt = sb.tile([P, w], F32, name="rt", tag="rt", bufs=4, align_bytes=64)
+            rv = rbfs[rows, c0 * KP : c0 * KP + w].rearrange("(p j) w -> p j w", j=J)
+            nc.sync.dma_start(out=rt[:], in_=rv[:, j, :])
+            r_t[u, j] = rt
 
         def load_dc(dst, src, g):
             nc.sync.dma_start(out=dst[:, g, :, :], in_=src[g * KP : (g + 1) * KP, :].rearrange("(p j) w -> p j w", j=J))
 
         def load_gd(g):
-            t = ldp.tile([P, J, D], BF16, name="gd", tag="gd", bufs=2, align_bytes=64)
+            t = sb.tile([P, J, D], BF16, name="gd", tag="o", bufs=5, align_bytes=64)
             nc.sync.dma_start(out=t[:], in_=grad_out[g * KP : (g + 1) * KP, 1 : 1 + D].rearrange("(p j) w -> p j w", j=J))
             gd_t[g] = t
 
-        def stt(s, j):
-            g, h = gh(s)
+        def stt(u, j):
+            g, c0, ncs = UNITS[u]
+            w = ncs * KP
             if j == 0:
-                dz_t[s] = dzp.tile([P, J, W], F32, name="dzt", tag="dzt", bufs=2, align_bytes=64)
+                dz_t[u] = sb.tile([P, J, w], F32, name="dzt", tag="dzt", bufs=3, align_bytes=64)
             nc.vector.scalar_tensor_tensor(
-                out=dz_t[s][:, j, :].rearrange("p (t q) -> p q t", t=J),
-                in0=g_t[s, j // 2][:, j % 2, :].rearrange("p (q t) -> p q t", t=J),
+                out=dz_t[u][:, j, :].rearrange("p (t q) -> p q t", t=J),
+                in0=g_t[u, j // 2][:, j % 2, :].rearrange("p (q t) -> p q t", t=J),
                 scalar=10.0,
-                in1=r_t[s, j // 2][:, j % 2, :].rearrange("p (q t) -> p q t", t=J),
+                in1=r_t[u, j][:].rearrange("p (q t) -> p q t", t=J),
                 op0=MULT, op1=MULT,
-                accum_out=rowp[:, g, h, j : j + 1],
+                accum_out=rowp[:, g, c0, j : j + 1],
             )
 
-        def transp(s, j):
-            for c in range(NC):
-                b = psz.tile([P, J, P], F32, name="zb", tag="zb", bufs=3)
+        def blk(u, c, t):
+            a = (t * UNITS[u][2] + c) * P
+            return slice(a, a + P)
+
+        def transp(u, j):
+            ncs = UNITS[u][2]
+            for c in range(ncs):
+                b = bank("zb", 3)
                 for t in range(J):
-                    a = t * (W // J) + c * P
-                    nc.tensor.transpose(b[:, t, :], dz_t[s][:, j, a : a + P], ident[:])
-                if (s, c) not in z_t:
-                    z_t[s, c] = mid.tile([P, J, P, J], BF16, name="zt", tag="zt", bufs=3, align_bytes=64)
-                nc.scalar.copy(z_t[s, c][:, j, :, :], b[:].rearrange("p t r -> p r t"))
+                    nc.tensor.transpose(b[:, t, :], dz_t[u][:, j, blk(u, c, t)], ident[:])
+                if u not in z_t:
+                    z_t[u] = sb.tile([P, ncs, J, P, J], BF16, name="zt", tag="zt", bufs=2, align_bytes=64)
+                nc.scalar.copy(z_t[u][:, c, j, :, :], b[:].rearrange("p t r -> p r t"))
 
-        def xpiece(s, k):
+        def xpiece(u, k, eng):
+            w = UNITS[u][2] * P
             if k % 2 == 0:
-                x_t[s, k // 2] = mid.tile([P, W // 2, J], BF16, name="xt", tag="xt", bufs=2, align_bytes=64)
-            w = W // 4
-            nc.scalar.copy(
-                x_t[s, k // 2][:, (k % 2) * w : (k % 2 + 1) * w, :].rearrange("p (c i) j -> p c j i", i=4),
-                dz_t[s][:, :, k * w : (k + 1) * w].rearrange("p j (c i) -> p c j i", i=4),
-            )
+                x_t[u, k // 2] = sb.tile([P, 2 * w, J], BF16, name="xt", tag="xt", bufs=2, align_bytes=64)
+            o = x_t[u, k // 2][:, (k % 2) * w : (k % 2 + 1) * w, :].rearrange("p (c i) j -> p c j i", i=4)
+            i_ = dz_t[u][:, :, k * w : (k + 1) * w].rearrange("p j (c i) -> p c j i", i=4)
+            if eng == 0:
+                nc.vector.tensor_copy(o, i_)
+            else:
+                nc.scalar.copy(o, i_)
 
-        def qz(s, c):
-            if c == 0:
-                zq[s] = cod.tile([P, NC, KP], U32, name="zqt", tag="zqt", bufs=6, align_bytes=64)
-                zs[s] = cod.tile([P, NC, KP], U8, name="zst", tag="zst", bufs=6, align_bytes=64)
-            nc.vector.quantize_mx(out=zq[s][:, c, :].bitcast(E5), scales=zs[s][:, c, :],
-                                  in_=z_t[s, c][:].rearrange("p j r t -> p (j r t)"))
+        def qz(u):
+            g, c0, ncs = UNITS[u]
+            q = sb.tile([P, ncs, KP], U32, name="zqt", tag="zqt", bufs=5, align_bytes=64)
+            s = sb.tile([P, ncs, KP], U8, name="zst", tag="zst", bufs=5, align_bytes=64)
+            nc.vector.quantize_mx(out=q[:].rearrange("p c r -> p (c r)").bitcast(E5), scales=s[:].rearrange("p c r -> p (c r)"),
+                                  in_=z_t[u][:].rearrange("p c j r t -> p (c j r t)"))
+            for c in range(ncs):
+                zloc[g, c0 + c] = (q, s, c)
+            if all((g, cc) in zloc for cc in range(NCC)):
+                nrow_f(g)
+                for j in range(J):
+                    todo.append((mx0, epi0, (g, j)))
 
-        def qx(s, k):
+        def xtag(u):
+            return "xa" if UNITS[u][1] == 0 or UNITS[u][2] == 1 else "xb"
+
+        def qx(u, k):
+            g, c0, ncs = UNITS[u]
+            w = ncs * KP
             if k == 0:
-                xq[s] = cod.tile([P, W], U32, name="xqt", tag="xqt", bufs=5, align_bytes=64)
-                xs[s] = cod.tile([P, W], U8, name="xst", tag="xst", bufs=5, align_bytes=64)
-            sl = slice(k * W // 2, (k + 1) * W // 2)
-            nc.vector.quantize_mx(out=xq[s][:, sl].bitcast(E5), scales=xs[s][:, sl],
-                                  in_=x_t[s, k][:].rearrange("p w j -> p (w j)"))
-
-        dc_t = {}
+                q = sb.tile([P, w], U32, name="xqt", tag=xtag(u), bufs=XQB[xtag(u)], align_bytes=64)
+                s = sb.tile([P, w], U8, name="xst", tag="s" + xtag(u), bufs=XQB[xtag(u)], align_bytes=64)
+                for c in range(ncs):
+                    xloc[g, c0 + c] = (q, s, u, c)
+            q, s = xloc[g, c0][:2]
+            sl = slice(k * w // 2, (k + 1) * w // 2)
+            nc.vector.quantize_mx(out=q[:, sl].bitcast(E5), scales=s[:, sl], in_=x_t[u, k][:].rearrange("p w j -> p (w j)"))
+            if k == 1:
+                if all((gg, c0) in xloc for gg in range(NG)):
+                    ncol_f(c0, ncs)
+                    for c in range(ncs):
+                        for t in range(J):
+                            todo.append((mx1, epi1, (c0 + c, t)))
 
         def dc_copy(name, src, g, eng):
-            t = mid.tile([P, D, J], BF16, name="dct", tag="dct", bufs=2, align_bytes=64)
+            t = sb.tile([P, D, J], BF16, name="dct", tag="o", bufs=5, align_bytes=64)
             o = t[:].rearrange("p (c i) j -> p c j i", i=4)
             i_ = src[:, g, :, :].rearrange("p j (c i) -> p c j i", i=4)
             if eng == 0:
@@ -143,137 +176,163 @@ def tile_dicgaussianrbf_v_kernel(tc, data, centers, rbfs, grad_out, out_0, out_1
             dc_t[name, g] = t
 
         def dc_quant(name, q, sc, g):
-            nc.vector.quantize_mx(out=q[:, g, :].bitcast(E4), scales=sc[:, g, :],
-                                  in_=dc_t[name, g][:].rearrange("p w j -> p (w j)"))
+            nc.vector.quantize_mx(out=q[:, g, :].bitcast(E4), scales=sc[:, g, :], in_=dc_t[name, g][:].rearrange("p w j -> p (w j)"))
 
-        def col_t(s):
-            for c in range(NC):
-                b = psc.tile([P, J, P], F32, name="cb", tag="cb", bufs=2)
+        def col_t(gi, c):
+            us = GROUPS[gi]
+            b = bank("cb", 2)
+            n = len(us) * J
+            for t in range(J):
+                for i in range(n):
+                    u = us[i // J]
+                    nc.tensor.matmul(b[:, t, :], lhsT=dz_t[u][:, i % J, blk(u, c, t)], rhs=ident[:],
+                                     is_transpose=True, start=(i == 0), stop=(i == n - 1))
+            col_b[gi, c] = b
+
+        def col_r(gi, c):
+            u = GROUPS[gi][-1]
+            cc = UNITS[u][1] + c
+            k = ncolg.get(cc, 0)
+            ncolg[cc] = k + 1
+            if gi in RS:
                 for t in range(J):
-                    a = t * (W // J) + c * P
-                    for j in range(J):
-                        nc.tensor.matmul(b[:, t, :], lhsT=dz_t[s][:, j, a : a + P], rhs=ident[:],
-                                         is_transpose=True, start=(j == 0), stop=(j == J - 1))
-                col_b[s, c] = b
-
-        def col_r(s):
-            g, h = gh(s)
-            for c in range(NC):
-                nc.vector.tensor_reduce(colp[:, h, c, g, :], col_b[s, c][:], AX, ADD)
+                    junk = sb.tile([P, P], BF16, name="junk", tag="junk", bufs=2, align_bytes=64)
+                    nc.scalar.activation(junk[:], col_b[gi, c][:, t, :], mybir.ActivationFunctionType.Copy, scale=-1.0,
+                                         accum_out=colp[:, cc, t, k : k + 1])
+            else:
+                nc.vector.tensor_reduce(colp[:, cc, :, k], col_b[gi, c][:], AX, ADD, negate=True)
 
         def nrow_f(g):
-            nc.vector.scalar_tensor_tensor(out=nrow[:, g, :], in0=rowp[:, g, 0, :], scalar=-1.0, in1=rowp[:, g, 1, :],
-                                           op0=MULT, op1=SUB)
+            starts = [c0 for (gg, c0, ncs) in UNITS if gg == g]
+            a = starts[0]
+            t = rowp[:, g, a, :]
+            if len(starts) > 2:
+                tt = keep.tile([P, J], F32, name="rtmp")
+                nc.vector.tensor_tensor(out=tt[:], in0=t, in1=rowp[:, g, starts[2], :], op=ADD)
+                t = tt[:]
+            nc.vector.scalar_tensor_tensor(out=nrow[:, g, :], in0=t, scalar=-1.0, in1=rowp[:, g, starts[1], :], op0=MULT, op1=SUB)
 
-        def ncol_f(h):
-            tmp = keep.tile([P, NC, J], F32, name="ctmp", tag="ctmp", bufs=1)
-            nc.vector.tensor_reduce(tmp[:], colp[:, h, :, :, :].rearrange("p c g t -> p c t g"), AX, ADD)
-            nc.vector.tensor_scalar(ncol[:, h, :, :], tmp[:], -1.0, None, op0=MULT)
+        def ncol_f(c0, ncs):
+            nc.vector.tensor_reduce(ncol[:, c0 : c0 + ncs, :], colp[:, c0 : c0 + ncs, :, :], AX, ADD)
 
-        def mx0(g, j):
-            b = psm.tile([P, D], F32, name="mb", tag="mb", bufs=3)
-            for cc in range(NH * NC):
-                s = (cc // NC) * NG + g
+        def mx0(b, g, j):
+            for cc in range(NCC):
+                q, s, c = zloc[g, cc]
                 nc.tensor.matmul_mx(
-                    out=b[:],
-                    lhsT=zq[s][:, cc % NC, j * P : (j + 1) * P].bitcast(E5),
-                    lhsT_scale=zs[s][:, cc % NC, j * P : (j + 1) * P],
+                    out=b, lhsT=q[:, c, j * P : (j + 1) * P].bitcast(E5), lhsT_scale=s[:, c, j * P : (j + 1) * P],
                     rhs=cent_q[:, cc, :].bitcast(E4), rhs_scale=cent_s[:, cc, :],
-                    start=(cc == 0), stop=(cc == NH * NC - 1))
-            mm0[g, j] = b
+                    start=(cc == 0), stop=(cc == NCC - 1))
 
-        def mx1(h, c, t):
-            b = psm.tile([P, D], F32, name="mb", tag="mb", bufs=3)
-            a = t * (W // J) + c * P
+        def mx1(b, cc, t):
             for g in range(NG):
-                s = h * NG + g
+                q, s, u, c = xloc[g, cc]
                 nc.tensor.matmul_mx(
-                    out=b[:],
-                    lhsT=xq[s][:, a : a + P].bitcast(E5), lhsT_scale=xs[s][:, a : a + P],
+                    out=b, lhsT=q[:, blk(u, c, t)].bitcast(E5), lhsT_scale=s[:, blk(u, c, t)],
                     rhs=data_q[:, g, :].bitcast(E4), rhs_scale=data_s[:, g, :],
                     start=(g == 0), stop=(g == NG - 1))
-            mm1[h, c, t] = b
 
-        def epi0a(g, j):
-            if j % 2 == 0:
-                ost[0, g, j // 2] = outp.tile([P, 2, D], F32, name="o", tag="o", bufs=4, align_bytes=64)
-            o = ost[0, g, j // 2]
+        def out_tile(key, i):
+            if i % 2 == 0:
+                ost[key] = sb.tile([P, 2, D], F32, name="o", tag="o", bufs=5, align_bytes=64)
+            return ost[key]
+
+        def store(dst, row, i, o):
+            nc.sync.dma_start(out=dst[row * KP : (row + 1) * KP, :].rearrange("(p j) w -> p j w", j=J)[:, i - 1 : i + 1, :], in_=o[:])
+
+        def epi0(b, g, j):
+            o = out_tile((0, g, j // 2), j)
             nc.vector.scalar_tensor_tensor(out=o[:, j % 2, :], in0=data_sb[:, g, j, :], scalar=nrow[:, g, j : j + 1],
-                                           in1=mm0[g, j][:], op0=MULT, op1=ADD)
+                                           in1=b, op0=MULT, op1=ADD)
+            if j % 2 == 1:
+                later.append((g, j, o))
 
-        def epi0b(g, jp):
-            o = ost[0, g, jp]
-            nc.vector.tensor_tensor(out=o[:], in0=o[:], in1=gd_t[g][:, 2 * jp : 2 * jp + 2, :], op=ADD)
-            nc.sync.dma_start(out=out_0[g * KP : (g + 1) * KP, :].rearrange("(p j) w -> p j w", j=J)[:, 2 * jp : 2 * jp + 2, :],
-                              in_=o[:])
+        def epi0b(g, j, o):
+            nc.vector.tensor_tensor(out=o[:], in0=o[:], in1=gd_t[g][:, j - 1 : j + 1, :], op=ADD)
+            store(out_0, g, j, o)
 
-        def epi1(h, c, t):
-            if t % 2 == 0:
-                ost[1, h, c, t // 2] = outp.tile([P, 2, D], F32, name="o", tag="o", bufs=4, align_bytes=64)
-            o = ost[1, h, c, t // 2]
-            cc = h * NC + c
-            nc.vector.scalar_tensor_tensor(out=o[:, t % 2, :], in0=cent_sb[:, cc, t, :], scalar=ncol[:, h, c, t : t + 1],
-                                           in1=mm1[h, c, t][:], op0=MULT, op1=ADD)
+        def epi1(b, cc, t):
+            o = out_tile((1, cc, t // 2), t)
+            nc.vector.scalar_tensor_tensor(out=o[:, t % 2, :], in0=cent_sb[:, cc, t, :], scalar=ncol[:, cc, t : t + 1],
+                                           in1=b, op0=MULT, op1=ADD)
             if t % 2 == 1:
-                tp = t // 2
-                nc.sync.dma_start(out=out_1[cc * KP : (cc + 1) * KP, :].rearrange("(p j) w -> p j w", j=J)[:, 2 * tp : 2 * tp + 2, :],
-                                  in_=o[:])
+                store(out_1, cc, t, o)
 
-        for s in range(UNITS + 1):
-            g, h = gh(s)
-            if s < UNITS:
-                load_unit(s, 0)
-                load_unit(s, 1)
-            if s < NG:
-                load_dc(data_sb, data, g)
-                load_dc(cent_sb, centers, g)
-            elif s < UNITS:
-                load_gd(g)
-            for j in range(J):
-                if s < UNITS:
-                    stt(s, j)
-                    if s >= 1:
-                        xpiece(s - 1, j)
-                    if j == 0 and s >= 1:
-                        col_t(s - 1)
-                    transp(s, j)
-                else:
-                    xpiece(s - 1, j)
-                    if j == 0:
-                        col_t(s - 1)
-                if s >= 1:
-                    if j < 2:
-                        qz(s - 1, j)
-                    if j == 2:
-                        col_r(s - 1)
-                        qx(s - 1, 0)
-                    if j == 3:
-                        qx(s - 1, 1)
-                if s < NG:
-                    if j == 1:
-                        dc_copy("d", data_sb, g, 0)
-                    if j == 2:
-                        dc_copy("c", cent_sb, g, 1)
-                        dc_quant("d", data_q, data_s, g)
-                    if j == 3:
-                        dc_quant("c", cent_q, cent_s, g)
-            if s > NG:
-                gp = (s - 1) % NG
-                nrow_f(gp)
+        todo, popped, later = [], [], []
+
+        def pop_jobs(n):
+            for i in range(n):
+                if todo:
+                    mxf, epf, args = todo.pop(0)
+                    b = ps.tile([P, D], F32, name="mb", tag="mb", bufs=3)
+                    mxf(b[:], *args)
+                    popped.append((epf, b, args))
+
+        def do_epis():
+            late = list(later)
+            later.clear()
+            for epf, b, args in popped:
+                epf(b[:], *args)
+            popped.clear()
+            for a in late:
+                epi0b(*a)
+
+        def group_of(u):
+            for gi in range(len(GROUPS)):
+                if GROUPS[gi][-1] == u:
+                    return gi
+            return None
+
+        C_V = (0, 1, 2, 3)
+        GD = {2: 0, 5: 1, 6: 2, 8: 3}
+
+        if True:
+            load_dc(cent_sb, centers, 0)
+            load_j(0)
+            load_dc(cent_sb, centers, 1)
+            load_j(1)
+            load_dc(cent_sb, centers, 2)
+            load_j(2)
+            load_j(3)
+            load_dc(cent_sb, centers, 3)
+            dc_copy("c", cent_sb, 0, 0)
+            for u in range(NU + 1):
                 for j in range(J):
-                    mx0(gp, j)
-                    epi0a(gp, j)
-                    if j % 2 == 1:
-                        epi0b(gp, j // 2)
-            if s == NG:
-                ncol_f(0)
-            if s == NG + 1 or s == NG + 2:
-                for t in range(J):
-                    mx1(0, s - NG - 1, t)
-                    epi1(0, s - NG - 1, t)
-            if s == UNITS:
-                ncol_f(1)
-                for c in range(NC):
-                    for t in range(J):
-                        mx1(1, c, t)
-                        epi1(1, c, t)
+                    pre = UNITS[u - 1][2] if u >= 1 else 0
+                    gi = group_of(u - 1)
+                    if u < NU:
+                        stt(u, j)
+                        load_j(J * u + j + 4)
+                    if u in (1, 2) and j in (0, 2):
+                        load_dc(data_sb, data, 2 * (u - 1) + j // 2)
+                    if gi is not None and j < pre:
+                        col_t(gi, j)
+                    if u >= 1:
+                        xpiece(u - 1, j, 0 if (u - 1, j) in XV or (u == NU and j % 2 == 1) else 1)
+                    if u < NU:
+                        transp(u, j)
+                    if u >= 1 and j == 1:
+                        qz(u - 1)
+                    if gi is not None and j == 2:
+                        for c in range(pre):
+                            col_r(gi, c)
+                    if u >= 1 and j == 3:
+                        qx(u - 1, 0)
+                        if u == NU:
+                            qx(u - 1, 1)
+                    if u >= 2 and j == 0:
+                        qx(u - 2, 1)
+                    if u == 0:
+                        if j < 3:
+                            dc_copy("c", cent_sb, j + 1, 0 if j + 1 in C_V else 1)
+                        dc_quant("c", cent_q, cent_s, j)
+                    if 1 <= u < 5 and j == 2:
+                        dc_copy("d", data_sb, u - 1, 0 if u - 1 in () else 1)
+                    if 2 <= u < 6 and j == 0:
+                        dc_quant("d", data_q, data_s, u - 2)
+                    do_epis()
+                    if j == 0 and u in GD:
+                        load_gd(GD[u])
+                    pop_jobs(2 if len(todo) > 3 else 1)
+            while todo or popped or later:
+                do_epis()
+                pop_jobs(2)

@@ -12,6 +12,7 @@ U32 = mybir.dt.uint32
 U8 = mybir.dt.uint8
 E4 = mybir.dt.float8_e4m3fn_x4
 E5 = mybir.dt.float8_e5m2_x4
+COPY = mybir.ActivationFunctionType.Copy
 MULT = mybir.AluOpType.mult
 ADD = mybir.AluOpType.add
 SUB = mybir.AluOpType.subtract
@@ -22,12 +23,13 @@ J = 4
 KP = P * J
 NG = N // KP
 NCC = K // KP
-UNITS = [(0, 2, 2), (0, 0, 2), (1, 0, 2), (2, 0, 2), (3, 0, 2), (1, 2, 2), (2, 2, 2), (3, 2, 1), (3, 3, 1)]
+NC = 2
+W = NC * KP
+NH = K // W
+UNITS = [(g, 0) for g in range(NG)] + [(g, 1) for g in range(NG)]
 NU = len(UNITS)
-XQB = {"xa": 4, "xb": 3}
-RS = (3, 4, 5)
-GROUPS = [(0,), (1, 2), (3, 4), (5, 6), (7,), (8,)]
-XV = ()
+RSV = (1,)
+XV = [(u, k) for u in range(4) for k in (2, 3)]
 
 
 def tile_dicgaussianrbf_v_kernel(tc, data, centers, rbfs, grad_out, out_0, out_1):
@@ -40,200 +42,155 @@ def tile_dicgaussianrbf_v_kernel(tc, data, centers, rbfs, grad_out, out_0, out_1
         ident = keep.tile([P, P], F32, name="ident")
         make_identity(nc, ident[:])
         warm = keep.tile([P, 1], F32, name="warm")
-        nc.vector.memset(warm[:], 0.0)
         nc.scalar.copy(warm[:], ident[:, 0:1])
 
         data_sb = keep.tile([P, NG, J, D], BF16, name="data_sb", align_bytes=64)
-        cent_sb = keep.tile([P, NG, J, D], BF16, name="cent_sb", align_bytes=64)
+        cent_sb = keep.tile([P, NCC, J, D], BF16, name="cent_sb", align_bytes=64)
         data_q = keep.tile([P, NG, D], U32, name="data_q", align_bytes=64)
         data_s = keep.tile([P, NG, D], U8, name="data_s", align_bytes=64)
-        cent_q = keep.tile([P, NG, D], U32, name="cent_q", align_bytes=64)
-        cent_s = keep.tile([P, NG, D], U8, name="cent_s", align_bytes=64)
-        rowp = keep.tile([P, NG, NCC, J], F32, name="rowp")
+        cent_q = keep.tile([P, NCC, D], U32, name="cent_q", align_bytes=64)
+        cent_s = keep.tile([P, NCC, D], U8, name="cent_s", align_bytes=64)
+        rowp = keep.tile([P, NG, NH, J], F32, name="rowp")
         nrow = keep.tile([P, NG, J], F32, name="nrow")
-        colp = keep.tile([P, NCC, J, 3], F32, name="colp")
         ncol = keep.tile([P, NCC, J], F32, name="ncol")
-        nc.vector.memset(colp[:], 0.0)
 
-        g_t, r_t, dz_t, x_t, z_t = {}, {}, {}, {}, {}
-        zloc, xloc, gd_t, col_b, dc_t, ost, ncolg = {}, {}, {}, {}, {}, {}, {}
+        g_t, r_t, dz_t, x_t, z_t, zq, xq = {}, {}, {}, {}, {}, {}, {}
+        gd_t, col_b, dc_t, ost = {}, {}, {}, {}
 
-        def bank(tag, bufs):
-            return ps.tile([P, J, P], F32, name=tag, tag=tag, bufs=bufs)
-
-        def load_j(n):
-            u, j = n // J, n % J
-            if u >= NU:
+        def load(n):
+            if n >= J * NU:
                 return
-            g, c0, ncs = UNITS[u]
-            w = ncs * KP
+            u, j = n // J, n % J
+            g, h = UNITS[u]
             rows = slice(g * KP, (g + 1) * KP)
+            gv = grad_out[rows, 1 + D + h * W : 1 + D + (h + 1) * W].rearrange("(p j) w -> p j w", j=J)
+            rv = rbfs[rows, h * W : (h + 1) * W].rearrange("(p j) w -> p j w", j=J)
             if j % 2 == 0:
-                gt = sb.tile([P, 2, w], BF16, name="gt", tag="gt", bufs=3, align_bytes=64)
-                g_t[u, j // 2] = gt
-                gv = grad_out[rows, 1 + D + c0 * KP : 1 + D + c0 * KP + w].rearrange("(p j) w -> p j w", j=J)
-                if n == 0:
-                    nc.sync.dma_start(out=gt[:, 0, :], in_=gv[:, 0, :])
-                else:
-                    nc.sync.dma_start(out=gt[:], in_=gv[:, j : j + 2, :])
-            elif n == 1:
-                gv = grad_out[rows, 1 + D + c0 * KP : 1 + D + c0 * KP + w].rearrange("(p j) w -> p j w", j=J)
-                nc.sync.dma_start(out=g_t[u, 0][:, 1, :], in_=gv[:, 1, :])
-            rt = sb.tile([P, w], F32, name="rt", tag="rt", bufs=4, align_bytes=64)
-            rv = rbfs[rows, c0 * KP : c0 * KP + w].rearrange("(p j) w -> p j w", j=J)
-            nc.sync.dma_start(out=rt[:], in_=rv[:, j, :])
-            r_t[u, j] = rt
+                g_t[u, j // 2] = sb.tile([P, 2, W], BF16, name="gt", tag="gt", bufs=3, align_bytes=64)
+            if n < 2:
+                nc.sync.dma_start(out=g_t[u, 0][:, j, :], in_=gv[:, j, :])
+            elif j % 2 == 0:
+                nc.sync.dma_start(out=g_t[u, j // 2][:], in_=gv[:, j : j + 2, :])
+            r_t[u, j] = sb.tile([P, W], F32, name="rt", tag="rt", bufs=4, align_bytes=64)
+            nc.sync.dma_start(out=r_t[u, j][:], in_=rv[:, j, :])
 
         def load_dc(dst, src, g):
             nc.sync.dma_start(out=dst[:, g, :, :], in_=src[g * KP : (g + 1) * KP, :].rearrange("(p j) w -> p j w", j=J))
 
         def load_gd(g):
-            t = sb.tile([P, J, D], BF16, name="gd", tag="o", bufs=5, align_bytes=64)
-            nc.sync.dma_start(out=t[:], in_=grad_out[g * KP : (g + 1) * KP, 1 : 1 + D].rearrange("(p j) w -> p j w", j=J))
-            gd_t[g] = t
+            gd_t[g] = sb.tile([P, J, D], BF16, name="gd", tag="o", bufs=6, align_bytes=64)
+            nc.sync.dma_start(out=gd_t[g][:], in_=grad_out[g * KP : (g + 1) * KP, 1 : 1 + D].rearrange("(p j) w -> p j w", j=J))
 
         def stt(u, j):
-            g, c0, ncs = UNITS[u]
-            w = ncs * KP
+            g, h = UNITS[u]
             if j == 0:
-                dz_t[u] = sb.tile([P, J, w], F32, name="dzt", tag="dzt", bufs=3, align_bytes=64)
+                dz_t[u] = sb.tile([P, J, W], F32, name="dzt", tag="dzt", bufs=3, align_bytes=64)
             nc.vector.scalar_tensor_tensor(
                 out=dz_t[u][:, j, :].rearrange("p (t q) -> p q t", t=J),
                 in0=g_t[u, j // 2][:, j % 2, :].rearrange("p (q t) -> p q t", t=J),
                 scalar=10.0,
                 in1=r_t[u, j][:].rearrange("p (q t) -> p q t", t=J),
-                op0=MULT, op1=MULT,
-                accum_out=rowp[:, g, c0, j : j + 1],
-            )
+                op0=MULT, op1=MULT, accum_out=rowp[:, g, h, j : j + 1])
 
-        def blk(u, c, t):
-            a = (t * UNITS[u][2] + c) * P
+        def blk(c, t):
+            a = (t * NC + c) * P
             return slice(a, a + P)
 
         def transp(u, j):
-            ncs = UNITS[u][2]
-            for c in range(ncs):
-                b = bank("zb", 3)
+            for c in range(NC):
+                b = ps.tile([P, J, P], F32, name="zb", tag="zb", bufs=2)
                 for t in range(J):
-                    nc.tensor.transpose(b[:, t, :], dz_t[u][:, j, blk(u, c, t)], ident[:])
+                    nc.tensor.transpose(b[:, t, :], dz_t[u][:, j, blk(c, t)], ident[:])
                 if u not in z_t:
-                    z_t[u] = sb.tile([P, ncs, J, P, J], BF16, name="zt", tag="zt", bufs=2, align_bytes=64)
-                nc.scalar.copy(z_t[u][:, c, j, :, :], b[:].rearrange("p t r -> p r t"))
+                    z_t[u] = sb.tile([P, NC, J, P, J], BF16, name="zt", tag="zt", bufs=2, align_bytes=64)
+                nc.scalar.copy(z_t[u][:, c, j, :, :].rearrange("p (r i) t -> p r t i", i=4),
+                               b[:].rearrange("p t (r i) -> p r t i", i=4))
 
-        def xpiece(u, k, eng):
-            w = UNITS[u][2] * P
-            if k % 2 == 0:
-                x_t[u, k // 2] = sb.tile([P, 2 * w, J], BF16, name="xt", tag="xt", bufs=2, align_bytes=64)
-            o = x_t[u, k // 2][:, (k % 2) * w : (k % 2 + 1) * w, :].rearrange("p (c i) j -> p c j i", i=4)
-            i_ = dz_t[u][:, :, k * w : (k + 1) * w].rearrange("p j (c i) -> p c j i", i=4)
+        def inter(eng, o, i_):
+            o = o.rearrange("p (c i) j -> p c j i", i=4)
+            i_ = i_.rearrange("p j (c i) -> p c j i", i=4)
             if eng == 0:
                 nc.vector.tensor_copy(o, i_)
             else:
                 nc.scalar.copy(o, i_)
 
+        def xpiece(u, k):
+            w = W // J
+            if k % 2 == 0:
+                x_t[u, k // 2] = sb.tile([P, W // 2, J], BF16, name="xt", tag="xt", bufs=2, align_bytes=64)
+            o = x_t[u, k // 2][:, (k % 2) * w : (k % 2 + 1) * w, :]
+            inter(0 if (u, k) in XV or (u == NU - 1 and k % 2 == 1 and 0) else 1, o, dz_t[u][:, :, k * w : (k + 1) * w])
+
         def qz(u):
-            g, c0, ncs = UNITS[u]
-            q = sb.tile([P, ncs, KP], U32, name="zqt", tag="zqt", bufs=5, align_bytes=64)
-            s = sb.tile([P, ncs, KP], U8, name="zst", tag="zst", bufs=5, align_bytes=64)
-            nc.vector.quantize_mx(out=q[:].rearrange("p c r -> p (c r)").bitcast(E5), scales=s[:].rearrange("p c r -> p (c r)"),
-                                  in_=z_t[u][:].rearrange("p c j r t -> p (c j r t)"))
-            for c in range(ncs):
-                zloc[g, c0 + c] = (q, s, c)
-            if all((g, cc) in zloc for cc in range(NCC)):
-                nrow_f(g)
+            g, h = UNITS[u]
+            q = sb.tile([P, W], U32, name="zqt", tag="zqt", bufs=6, align_bytes=64)
+            s = sb.tile([P, W], U8, name="zst", tag="zst", bufs=6, align_bytes=64)
+            nc.vector.quantize_mx(out=q[:].bitcast(E5), scales=s[:], in_=z_t[u][:].rearrange("p c j r t -> p (c j r t)"))
+            zq[g, h] = (q, s)
+            if (g, 1 - h) in zq:
+                nc.vector.scalar_tensor_tensor(out=nrow[:, g, :], in0=rowp[:, g, 0, :], scalar=-1.0, in1=rowp[:, g, 1, :], op0=MULT, op1=SUB)
                 for j in range(J):
                     todo.append((mx0, epi0, (g, j)))
 
-        def xtag(u):
-            return "xa" if UNITS[u][1] == 0 or UNITS[u][2] == 1 else "xb"
-
         def qx(u, k):
-            g, c0, ncs = UNITS[u]
-            w = ncs * KP
+            g, h = UNITS[u]
             if k == 0:
-                q = sb.tile([P, w], U32, name="xqt", tag=xtag(u), bufs=XQB[xtag(u)], align_bytes=64)
-                s = sb.tile([P, w], U8, name="xst", tag="s" + xtag(u), bufs=XQB[xtag(u)], align_bytes=64)
-                for c in range(ncs):
-                    xloc[g, c0 + c] = (q, s, u, c)
-            q, s = xloc[g, c0][:2]
-            sl = slice(k * w // 2, (k + 1) * w // 2)
+                q = sb.tile([P, W], U32, name="xqt", tag="xqt", bufs=5, align_bytes=64)
+                s = sb.tile([P, W], U8, name="xst", tag="xst", bufs=5, align_bytes=64)
+                xq[g, h] = (q, s)
+            q, s = xq[g, h]
+            sl = slice(k * W // 2, (k + 1) * W // 2)
             nc.vector.quantize_mx(out=q[:, sl].bitcast(E5), scales=s[:, sl], in_=x_t[u, k][:].rearrange("p w j -> p (w j)"))
-            if k == 1:
-                if all((gg, c0) in xloc for gg in range(NG)):
-                    ncol_f(c0, ncs)
-                    for c in range(ncs):
-                        for t in range(J):
-                            todo.append((mx1, epi1, (c0 + c, t)))
+            if k == 1 and g == NG - 1:
+                for c in range(NC):
+                    for t in range(J):
+                        todo.append((mx1, epi1, (h, c, t)))
 
         def dc_copy(name, src, g, eng):
-            t = sb.tile([P, D, J], BF16, name="dct", tag="o", bufs=5, align_bytes=64)
-            o = t[:].rearrange("p (c i) j -> p c j i", i=4)
-            i_ = src[:, g, :, :].rearrange("p j (c i) -> p c j i", i=4)
-            if eng == 0:
-                nc.vector.tensor_copy(o, i_)
-            else:
-                nc.scalar.copy(o, i_)
-            dc_t[name, g] = t
+            dc_t[name, g] = sb.tile([P, D, J], BF16, name="dct", tag="o", bufs=6, align_bytes=64)
+            inter(eng, dc_t[name, g][:], src[:, g, :, :])
 
         def dc_quant(name, q, sc, g):
             nc.vector.quantize_mx(out=q[:, g, :].bitcast(E4), scales=sc[:, g, :], in_=dc_t[name, g][:].rearrange("p w j -> p (w j)"))
 
-        def col_t(gi, c):
-            us = GROUPS[gi]
-            b = bank("cb", 2)
-            n = len(us) * J
+        def col_t(u, c):
+            g, h = UNITS[u]
+            if g == 0:
+                col_b[h, c] = ps.tile([P, J, P], F32, name="cb", tag="cb", bufs=2)
             for t in range(J):
-                for i in range(n):
-                    u = us[i // J]
-                    nc.tensor.matmul(b[:, t, :], lhsT=dz_t[u][:, i % J, blk(u, c, t)], rhs=ident[:],
-                                     is_transpose=True, start=(i == 0), stop=(i == n - 1))
-            col_b[gi, c] = b
+                for j in range(J):
+                    nc.tensor.matmul(col_b[h, c][:, t, :], lhsT=dz_t[u][:, j, blk(c, t)], rhs=ident[:], is_transpose=True,
+                                     start=(g == 0 and t == 0 and j == 0), stop=(g == NG - 1 and t == J - 1 and j == J - 1))
 
-        def col_r(gi, c):
-            u = GROUPS[gi][-1]
-            cc = UNITS[u][1] + c
-            k = ncolg.get(cc, 0)
-            ncolg[cc] = k + 1
-            if gi in RS:
+        def col_r(h, c):
+            cc = h * NC + c
+            if h in RSV:
                 for t in range(J):
                     junk = sb.tile([P, P], BF16, name="junk", tag="junk", bufs=2, align_bytes=64)
-                    nc.scalar.activation(junk[:], col_b[gi, c][:, t, :], mybir.ActivationFunctionType.Copy, scale=-1.0,
-                                         accum_out=colp[:, cc, t, k : k + 1])
+                    nc.scalar.activation(junk[:], col_b[h, c][:, t, :], COPY, scale=-1.0, accum_out=ncol[:, cc, t : t + 1])
             else:
-                nc.vector.tensor_reduce(colp[:, cc, :, k], col_b[gi, c][:], AX, ADD, negate=True)
-
-        def nrow_f(g):
-            starts = [c0 for (gg, c0, ncs) in UNITS if gg == g]
-            a = starts[0]
-            t = rowp[:, g, a, :]
-            if len(starts) > 2:
-                tt = keep.tile([P, J], F32, name="rtmp")
-                nc.vector.tensor_tensor(out=tt[:], in0=t, in1=rowp[:, g, starts[2], :], op=ADD)
-                t = tt[:]
-            nc.vector.scalar_tensor_tensor(out=nrow[:, g, :], in0=t, scalar=-1.0, in1=rowp[:, g, starts[1], :], op0=MULT, op1=SUB)
-
-        def ncol_f(c0, ncs):
-            nc.vector.tensor_reduce(ncol[:, c0 : c0 + ncs, :], colp[:, c0 : c0 + ncs, :, :], AX, ADD)
+                nc.vector.tensor_reduce(ncol[:, cc, :], col_b[h, c][:], AX, ADD, negate=True)
 
         def mx0(b, g, j):
             for cc in range(NCC):
-                q, s, c = zloc[g, cc]
+                q, s = zq[g, cc // NC]
+                a = (cc % NC) * KP + j * P
                 nc.tensor.matmul_mx(
-                    out=b, lhsT=q[:, c, j * P : (j + 1) * P].bitcast(E5), lhsT_scale=s[:, c, j * P : (j + 1) * P],
+                    out=b, lhsT=q[:, a : a + P].bitcast(E5), lhsT_scale=s[:, a : a + P],
                     rhs=cent_q[:, cc, :].bitcast(E4), rhs_scale=cent_s[:, cc, :],
                     start=(cc == 0), stop=(cc == NCC - 1))
 
-        def mx1(b, cc, t):
+        def mx1(b, h, c, t):
             for g in range(NG):
-                q, s, u, c = xloc[g, cc]
+                q, s = xq[g, h]
                 nc.tensor.matmul_mx(
-                    out=b, lhsT=q[:, blk(u, c, t)].bitcast(E5), lhsT_scale=s[:, blk(u, c, t)],
+                    out=b, lhsT=q[:, blk(c, t)].bitcast(E5), lhsT_scale=s[:, blk(c, t)],
                     rhs=data_q[:, g, :].bitcast(E4), rhs_scale=data_s[:, g, :],
                     start=(g == 0), stop=(g == NG - 1))
 
         def out_tile(key, i):
             if i % 2 == 0:
-                ost[key] = sb.tile([P, 2, D], F32, name="o", tag="o", bufs=5, align_bytes=64)
+                ost[key] = sb.tile([P, 2, D], F32, name="o", tag="o", bufs=6, align_bytes=64)
             return ost[key]
 
         def store(dst, row, i, o):
@@ -250,7 +207,8 @@ def tile_dicgaussianrbf_v_kernel(tc, data, centers, rbfs, grad_out, out_0, out_1
             nc.vector.tensor_tensor(out=o[:], in0=o[:], in1=gd_t[g][:, j - 1 : j + 1, :], op=ADD)
             store(out_0, g, j, o)
 
-        def epi1(b, cc, t):
+        def epi1(b, h, c, t):
+            cc = h * NC + c
             o = out_tile((1, cc, t // 2), t)
             nc.vector.scalar_tensor_tensor(out=o[:, t % 2, :], in0=cent_sb[:, cc, t, :], scalar=ncol[:, cc, t : t + 1],
                                            in1=b, op0=MULT, op1=ADD)
@@ -263,7 +221,9 @@ def tile_dicgaussianrbf_v_kernel(tc, data, centers, rbfs, grad_out, out_0, out_1
             for i in range(n):
                 if todo:
                     mxf, epf, args = todo.pop(0)
-                    b = ps.tile([P, D], F32, name="mb", tag="mb", bufs=3)
+                    if mxf is mx0 and args[1] == 0:
+                        load_gd(args[0])
+                    b = ps.tile([P, D], F32, name="mb", tag="mb", bufs=4)
                     mxf(b[:], *args)
                     popped.append((epf, b, args))
 
@@ -276,45 +236,41 @@ def tile_dicgaussianrbf_v_kernel(tc, data, centers, rbfs, grad_out, out_0, out_1
             for a in late:
                 epi0b(*a)
 
-        def group_of(u):
-            for gi in range(len(GROUPS)):
-                if GROUPS[gi][-1] == u:
-                    return gi
-            return None
-
-        C_V = (0, 1, 2, 3)
-        GD = {2: 0, 5: 1, 6: 2, 8: 3}
-
-        if True:
-            load_dc(cent_sb, centers, 0)
-            load_j(0)
-            load_dc(cent_sb, centers, 1)
-            load_j(1)
-            load_dc(cent_sb, centers, 2)
-            load_j(2)
-            load_j(3)
-            load_dc(cent_sb, centers, 3)
-            dc_copy("c", cent_sb, 0, 0)
+        C_AT = (6, 8, 10, 12)
+        D_V = (0, 1, 2, 3)
+        with tc.manual_schedule():
+            load_dc(data_sb, data, 0)
+            load(0)
+            load_dc(data_sb, data, 1)
+            load(1)
+            load_dc(data_sb, data, 2)
+            load(2)
+            load(3)
+            load_dc(data_sb, data, 3)
+            for n in range(4, 4):
+                load(n)
+            dc_copy("d", data_sb, 0, 0)
             for u in range(NU + 1):
                 for j in range(J):
-                    pre = UNITS[u - 1][2] if u >= 1 else 0
-                    gi = group_of(u - 1)
+                    n = J * u + j
                     if u < NU:
                         stt(u, j)
-                        load_j(J * u + j + 4)
-                    if u in (1, 2) and j in (0, 2):
-                        load_dc(data_sb, data, 2 * (u - 1) + j // 2)
-                    if gi is not None and j < pre:
-                        col_t(gi, j)
+                        load(n + 4)
+                    do_epis()
+                    pop_jobs(2 if len(todo) > 3 else 1)
+                    if n in C_AT:
+                        load_dc(cent_sb, centers, C_AT.index(n))
+                    if u >= 1 and j in (0, 2):
+                        col_t(u - 1, (0, 2).index(j))
                     if u >= 1:
-                        xpiece(u - 1, j, 0 if (u - 1, j) in XV or (u == NU and j % 2 == 1) else 1)
+                        xpiece(u - 1, j)
                     if u < NU:
                         transp(u, j)
-                    if u >= 1 and j == 1:
+                    if u >= 1 and j == 2:
                         qz(u - 1)
-                    if gi is not None and j == 2:
-                        for c in range(pre):
-                            col_r(gi, c)
+                    if u >= 1 and j == 3 and UNITS[u - 1][0] == NG - 1:
+                        for c in range(NC):
+                            col_r(UNITS[u - 1][1], c)
                     if u >= 1 and j == 3:
                         qx(u - 1, 0)
                         if u == NU:
@@ -323,16 +279,13 @@ def tile_dicgaussianrbf_v_kernel(tc, data, centers, rbfs, grad_out, out_0, out_1
                         qx(u - 2, 1)
                     if u == 0:
                         if j < 3:
-                            dc_copy("c", cent_sb, j + 1, 0 if j + 1 in C_V else 1)
-                        dc_quant("c", cent_q, cent_s, j)
-                    if 1 <= u < 5 and j == 2:
-                        dc_copy("d", data_sb, u - 1, 0 if u - 1 in () else 1)
-                    if 2 <= u < 6 and j == 0:
-                        dc_quant("d", data_q, data_s, u - 2)
-                    do_epis()
-                    if j == 0 and u in GD:
-                        load_gd(GD[u])
-                    pop_jobs(2 if len(todo) > 3 else 1)
+                            dc_copy("d", data_sb, j + 1, 0 if j + 1 in D_V else 1)
+                        dc_quant("d", data_q, data_s, j)
+                    if n - 4 in C_AT:
+                        dc_copy("c", cent_sb, C_AT.index(n - 4), 1)
+                    if n - 6 in C_AT:
+                        dc_quant("c", cent_q, cent_s, C_AT.index(n - 6))
+                    pass
             while todo or popped or later:
                 do_epis()
                 pop_jobs(2)

@@ -10,282 +10,322 @@ F32 = mybir.dt.float32
 BF16 = mybir.dt.bfloat16
 U32 = mybir.dt.uint32
 U8 = mybir.dt.uint8
-E4 = mybir.dt.float8_e4m3fn_x4
-E5 = mybir.dt.float8_e5m2_x4
+E4M3X4 = mybir.dt.float8_e4m3fn_x4
+E5M2X4 = mybir.dt.float8_e5m2_x4
 COPY = mybir.ActivationFunctionType.Copy
 MULT = mybir.AluOpType.mult
 ADD = mybir.AluOpType.add
 SUB = mybir.AluOpType.subtract
-AX = mybir.AxisListType.X
+AXIS_X = mybir.AxisListType.X
 
 P = 128
-J = 4
-KP = P * J
-NG = N // KP
-NCC = K // KP
-NC = 2
-W = NC * KP
-NH = K // W
-UNITS = [(g, 0) for g in range(NG)] + [(g, 1) for g in range(NG)]
-NU = len(UNITS)
-RSV = (1,)
-XV = [(u, k) for u in range(4) for k in (2, 3)]
+SLOTS = 4
+PASS = P * SLOTS
+ROW_BLOCKS = N // PASS
+CENTER_BLOCKS = K // PASS
+HALF_BLOCKS = 2
+HALF = HALF_BLOCKS * PASS
+HALVES = K // HALF
+PIECE = HALF // SLOTS
+
+UNITS = [(g, h) for h in range(HALVES) for g in range(ROW_BLOCKS)]
+FIRST_HALF_END = ROW_BLOCKS - 1
+
+VECTOR_PIECES = [(0, 3), (1, 0), (1, 2), (2, 3), (3, 0), (3, 2)]
+VECTOR_DATA = (0, 2)
+
+CENTER_STEPS = (12, 14, 16, 17)
+COPY_DELAY = 4
+QUANTIZE_DELAY = 6
+
+LOAD_AHEAD = 4
+BACKLOG = 6
+
+GRAD_BUFS, RBF_BUFS, DZ_BUFS = 3, 4, 3
+Z_BUFS, X_BUFS, Z_CODE_BUFS, X_CODE_BUFS = 2, 3, 6, 5
+STAGE_BUFS = 6
+TRANSPOSE_BANKS, COLUMN_BANKS, PRODUCT_BANKS = 3, 2, 3
 
 
 def tile_dicgaussianrbf_v_kernel(tc, data, centers, rbfs, grad_out, out_0, out_1):
     nc = tc.nc
     with ExitStack() as ctx:
         keep = ctx.enter_context(tc.tile_pool(name="keep", bufs=1))
-        sb = ctx.enter_context(tc.tile_pool(name="sb", bufs=1))
-        ps = ctx.enter_context(tc.psum_pool(name="ps", bufs=1))
+        work = ctx.enter_context(tc.tile_pool(name="work", bufs=1))
+        psum = ctx.enter_context(tc.psum_pool(name="psum", bufs=1))
 
-        ident = keep.tile([P, P], F32, name="ident")
-        make_identity(nc, ident[:])
-        warm = keep.tile([P, 1], F32, name="warm")
-        nc.scalar.copy(warm[:], ident[:, 0:1])
+        identity = keep.tile([P, P], F32, name="identity")
+        make_identity(nc, identity[:])
+        first_copy = keep.tile([P, 1], F32, name="first_copy")
+        nc.scalar.copy(first_copy[:], identity[:, 0:1])
 
-        data_sb = keep.tile([P, NG, J, D], BF16, name="data_sb", align_bytes=64)
-        cent_sb = keep.tile([P, NCC, J, D], BF16, name="cent_sb", align_bytes=64)
-        data_q = keep.tile([P, NG, D], U32, name="data_q", align_bytes=64)
-        data_s = keep.tile([P, NG, D], U8, name="data_s", align_bytes=64)
-        cent_q = keep.tile([P, NCC, D], U32, name="cent_q", align_bytes=64)
-        cent_s = keep.tile([P, NCC, D], U8, name="cent_s", align_bytes=64)
-        rowp = keep.tile([P, NG, NH, J], F32, name="rowp")
-        nrow = keep.tile([P, NG, J], F32, name="nrow")
-        ncol = keep.tile([P, NCC, J], F32, name="ncol")
+        data_sb = keep.tile([P, ROW_BLOCKS, SLOTS, D], BF16, name="data_sb", align_bytes=64)
+        centers_sb = keep.tile([P, CENTER_BLOCKS, SLOTS, D], BF16, name="centers_sb", align_bytes=64)
+        data_codes = keep.tile([P, ROW_BLOCKS, D], U32, name="data_codes", align_bytes=64)
+        data_scales = keep.tile([P, ROW_BLOCKS, D], U8, name="data_scales", align_bytes=64)
+        centers_codes = keep.tile([P, CENTER_BLOCKS, D], U32, name="centers_codes", align_bytes=64)
+        centers_scales = keep.tile([P, CENTER_BLOCKS, D], U8, name="centers_scales", align_bytes=64)
+        row_parts = keep.tile([P, ROW_BLOCKS, HALVES, SLOTS], F32, name="row_parts")
+        minus_row = keep.tile([P, ROW_BLOCKS, SLOTS], F32, name="minus_row")
+        minus_col = keep.tile([P, CENTER_BLOCKS, SLOTS], F32, name="minus_col")
 
-        g_t, r_t, dz_t, x_t, z_t, zq, xq = {}, {}, {}, {}, {}, {}, {}
-        gd_t, col_b, dc_t, ost = {}, {}, {}, {}
+        grad, rbf, dz, x, z, z_quantized, x_quantized = {}, {}, {}, {}, {}, {}, {}
+        g_data, column_bank, grouped, result = {}, {}, {}, {}
+        full_banks = []
+        waiting = []
+        started = []
+        half_done = []
 
-        def load(n):
-            if n >= J * NU:
+        def load_step(step):
+            u, j = step // SLOTS, step % SLOTS
+            if u == len(UNITS):
                 return
-            u, j = n // J, n % J
             g, h = UNITS[u]
-            rows = slice(g * KP, (g + 1) * KP)
-            gv = grad_out[rows, 1 + D + h * W : 1 + D + (h + 1) * W].rearrange("(p j) w -> p j w", j=J)
-            rv = rbfs[rows, h * W : (h + 1) * W].rearrange("(p j) w -> p j w", j=J)
+            rows = slice(g * PASS, (g + 1) * PASS)
+            grad_cols = slice(1 + D + h * HALF, 1 + D + (h + 1) * HALF)
+            grad_rows = grad_out[rows, grad_cols].rearrange("(p j) w -> p j w", j=SLOTS)
+            rbf_rows = rbfs[rows, h * HALF : (h + 1) * HALF].rearrange("(p j) w -> p j w", j=SLOTS)
             if j % 2 == 0:
-                g_t[u, j // 2] = sb.tile([P, 2, W], BF16, name="gt", tag="gt", bufs=3, align_bytes=64)
-            if n < 2:
-                nc.sync.dma_start(out=g_t[u, 0][:, j, :], in_=gv[:, j, :])
+                grad[u, j // 2] = work.tile([P, 2, HALF], BF16, name="grad", tag="grad", bufs=GRAD_BUFS, align_bytes=64)
+            if step < 2:
+                nc.sync.dma_start(out=grad[u, 0][:, j, :], in_=grad_rows[:, j, :])
             elif j % 2 == 0:
-                nc.sync.dma_start(out=g_t[u, j // 2][:], in_=gv[:, j : j + 2, :])
-            r_t[u, j] = sb.tile([P, W], F32, name="rt", tag="rt", bufs=4, align_bytes=64)
-            nc.sync.dma_start(out=r_t[u, j][:], in_=rv[:, j, :])
+                nc.sync.dma_start(out=grad[u, j // 2][:], in_=grad_rows[:, j : j + 2, :])
+            rbf[u, j] = work.tile([P, HALF], F32, name="rbf", tag="rbf", bufs=RBF_BUFS, align_bytes=64)
+            nc.sync.dma_start(out=rbf[u, j][:], in_=rbf_rows[:, j, :])
 
-        def load_dc(dst, src, g):
-            nc.sync.dma_start(out=dst[:, g, :, :], in_=src[g * KP : (g + 1) * KP, :].rearrange("(p j) w -> p j w", j=J))
+        def load_block(dst, src, b):
+            rows = src[b * PASS : (b + 1) * PASS, :]
+            nc.sync.dma_start(out=dst[:, b, :, :], in_=rows.rearrange("(p j) w -> p j w", j=SLOTS))
 
-        def load_gd(g):
-            gd_t[g] = sb.tile([P, J, D], BF16, name="gd", tag="o", bufs=6, align_bytes=64)
-            nc.sync.dma_start(out=gd_t[g][:], in_=grad_out[g * KP : (g + 1) * KP, 1 : 1 + D].rearrange("(p j) w -> p j w", j=J))
+        def load_g_data(g):
+            g_data[g] = work.tile([P, SLOTS, D], BF16, name="g_data", tag="stage", bufs=STAGE_BUFS, align_bytes=64)
+            rows = grad_out[g * PASS : (g + 1) * PASS, 1 : 1 + D]
+            nc.sync.dma_start(out=g_data[g][:], in_=rows.rearrange("(p j) w -> p j w", j=SLOTS))
 
-        def stt(u, j):
+        def compute_dz(u, j):
             g, h = UNITS[u]
             if j == 0:
-                dz_t[u] = sb.tile([P, J, W], F32, name="dzt", tag="dzt", bufs=3, align_bytes=64)
+                dz[u] = work.tile([P, SLOTS, HALF], F32, name="dz", tag="dz", bufs=DZ_BUFS, align_bytes=64)
             nc.vector.scalar_tensor_tensor(
-                out=dz_t[u][:, j, :].rearrange("p (t q) -> p q t", t=J),
-                in0=g_t[u, j // 2][:, j % 2, :].rearrange("p (q t) -> p q t", t=J),
+                out=dz[u][:, j, :].rearrange("p (t q) -> p q t", t=SLOTS),
+                in0=grad[u, j // 2][:, j % 2, :].rearrange("p (q t) -> p q t", t=SLOTS),
                 scalar=10.0,
-                in1=r_t[u, j][:].rearrange("p (q t) -> p q t", t=J),
-                op0=MULT, op1=MULT, accum_out=rowp[:, g, h, j : j + 1])
+                in1=rbf[u, j][:].rearrange("p (q t) -> p q t", t=SLOTS),
+                op0=MULT, op1=MULT, accum_out=row_parts[:, g, h, j : j + 1])
 
-        def blk(c, t):
-            a = (t * NC + c) * P
-            return slice(a, a + P)
+        def columns(c, t):
+            first = (t * HALF_BLOCKS + c) * P
+            return slice(first, first + P)
 
-        def transp(u, j):
-            for c in range(NC):
-                b = ps.tile([P, J, P], F32, name="zb", tag="zb", bufs=2)
-                for t in range(J):
-                    nc.tensor.transpose(b[:, t, :], dz_t[u][:, j, blk(c, t)], ident[:])
-                if u not in z_t:
-                    z_t[u] = sb.tile([P, NC, J, P, J], BF16, name="zt", tag="zt", bufs=2, align_bytes=64)
-                nc.scalar.copy(z_t[u][:, c, j, :, :].rearrange("p (r i) t -> p r t i", i=4),
-                               b[:].rearrange("p t (r i) -> p r t i", i=4))
+        def transpose_dz(u, j):
+            for c in range(HALF_BLOCKS):
+                bank = psum.tile([P, SLOTS, P], F32, name="transposed", tag="transposed", bufs=TRANSPOSE_BANKS)
+                for t in range(SLOTS):
+                    nc.tensor.transpose(bank[:, t, :], dz[u][:, j, columns(c, t)], identity[:])
+                full_banks.append((u, c, j, bank))
 
-        def inter(eng, o, i_):
-            o = o.rearrange("p (c i) j -> p c j i", i=4)
-            i_ = i_.rearrange("p j (c i) -> p c j i", i=4)
-            if eng == 0:
-                nc.vector.tensor_copy(o, i_)
+        def copy_out_transposed():
+            while full_banks:
+                u, c, j, bank = full_banks.pop(0)
+                if u not in z:
+                    z[u] = work.tile([P, HALF_BLOCKS, SLOTS, P, SLOTS], BF16, name="z", tag="z", bufs=Z_BUFS, align_bytes=64)
+                nc.scalar.copy(z[u][:, c, j, :, :].rearrange("p (r i) t -> p r t i", i=4),
+                               bank[:].rearrange("p t (r i) -> p r t i", i=4))
+
+        def interleave(on_vector, out, in_):
+            out = out.rearrange("p (c i) j -> p c j i", i=4)
+            in_ = in_.rearrange("p j (c i) -> p c j i", i=4)
+            if on_vector:
+                nc.vector.tensor_copy(out, in_)
             else:
-                nc.scalar.copy(o, i_)
+                nc.scalar.copy(out, in_)
 
-        def xpiece(u, k):
-            w = W // J
+        def interleave_piece(u, k):
             if k % 2 == 0:
-                x_t[u, k // 2] = sb.tile([P, W // 2, J], BF16, name="xt", tag="xt", bufs=2, align_bytes=64)
-            o = x_t[u, k // 2][:, (k % 2) * w : (k % 2 + 1) * w, :]
-            inter(0 if (u, k) in XV or (u == NU - 1 and k % 2 == 1 and 0) else 1, o, dz_t[u][:, :, k * w : (k + 1) * w])
+                x[u, k // 2] = work.tile([P, 2 * PIECE, SLOTS], BF16, name="x", tag="x", bufs=X_BUFS, align_bytes=64)
+            first = (k % 2) * PIECE
+            interleave((u, k) in VECTOR_PIECES, x[u, k // 2][:, first : first + PIECE, :],
+                       dz[u][:, :, k * PIECE : (k + 1) * PIECE])
 
-        def qz(u):
+        def interleave_block(on_vector, name, src, b):
+            grouped[name, b] = work.tile([P, D, SLOTS], BF16, name="grouped", tag="stage", bufs=STAGE_BUFS, align_bytes=64)
+            interleave(on_vector, grouped[name, b][:], src[:, b, :, :])
+
+        def quantize_block(name, codes, scales, b):
+            nc.vector.quantize_mx(out=codes[:, b, :].bitcast(E4M3X4), scales=scales[:, b, :],
+                                  in_=grouped[name, b][:].rearrange("p w j -> p (w j)"))
+
+        def quantize_by_centers(u):
             g, h = UNITS[u]
-            q = sb.tile([P, W], U32, name="zqt", tag="zqt", bufs=6, align_bytes=64)
-            s = sb.tile([P, W], U8, name="zst", tag="zst", bufs=6, align_bytes=64)
-            nc.vector.quantize_mx(out=q[:].bitcast(E5), scales=s[:], in_=z_t[u][:].rearrange("p c j r t -> p (c j r t)"))
-            zq[g, h] = (q, s)
-            if (g, 1 - h) in zq:
-                nc.vector.scalar_tensor_tensor(out=nrow[:, g, :], in0=rowp[:, g, 0, :], scalar=-1.0, in1=rowp[:, g, 1, :], op0=MULT, op1=SUB)
-                for j in range(J):
-                    todo.append((mx0, epi0, (g, j)))
+            codes = work.tile([P, HALF], U32, name="z_codes", tag="z_codes", bufs=Z_CODE_BUFS, align_bytes=64)
+            scales = work.tile([P, HALF], U8, name="z_scales", tag="z_scales", bufs=Z_CODE_BUFS, align_bytes=64)
+            nc.vector.quantize_mx(out=codes[:].bitcast(E5M2X4), scales=scales[:],
+                                  in_=z[u][:].rearrange("p c j r t -> p (c j r t)"))
+            z_quantized[g, h] = (codes, scales)
+            if h == HALVES - 1:
+                nc.vector.scalar_tensor_tensor(out=minus_row[:, g, :], in0=row_parts[:, g, 0, :], scalar=-1.0,
+                                               in1=row_parts[:, g, 1, :], op0=MULT, op1=SUB)
+                for j in range(SLOTS):
+                    waiting.append((multiply_0, finish_0, (g, j)))
 
-        def qx(u, k):
+        def quantize_by_tokens(u, part):
             g, h = UNITS[u]
-            if k == 0:
-                q = sb.tile([P, W], U32, name="xqt", tag="xqt", bufs=5, align_bytes=64)
-                s = sb.tile([P, W], U8, name="xst", tag="xst", bufs=5, align_bytes=64)
-                xq[g, h] = (q, s)
-            q, s = xq[g, h]
-            sl = slice(k * W // 2, (k + 1) * W // 2)
-            nc.vector.quantize_mx(out=q[:, sl].bitcast(E5), scales=s[:, sl], in_=x_t[u, k][:].rearrange("p w j -> p (w j)"))
-            if k == 1 and g == NG - 1:
-                for c in range(NC):
-                    for t in range(J):
-                        todo.append((mx1, epi1, (h, c, t)))
+            if part == 0:
+                codes = work.tile([P, HALF], U32, name="x_codes", tag="x_codes", bufs=X_CODE_BUFS, align_bytes=64)
+                scales = work.tile([P, HALF], U8, name="x_scales", tag="x_scales", bufs=X_CODE_BUFS, align_bytes=64)
+                x_quantized[g, h] = (codes, scales)
+            codes, scales = x_quantized[g, h]
+            cols = slice(part * HALF // 2, (part + 1) * HALF // 2)
+            nc.vector.quantize_mx(out=codes[:, cols].bitcast(E5M2X4), scales=scales[:, cols],
+                                  in_=x[u, part][:].rearrange("p w j -> p (w j)"))
+            if part == 1 and g == ROW_BLOCKS - 1:
+                for c in range(HALF_BLOCKS):
+                    for t in range(SLOTS):
+                        waiting.append((multiply_1, finish_1, (h, c, t)))
 
-        def dc_copy(name, src, g, eng):
-            dc_t[name, g] = sb.tile([P, D, J], BF16, name="dct", tag="o", bufs=6, align_bytes=64)
-            inter(eng, dc_t[name, g][:], src[:, g, :, :])
-
-        def dc_quant(name, q, sc, g):
-            nc.vector.quantize_mx(out=q[:, g, :].bitcast(E4), scales=sc[:, g, :], in_=dc_t[name, g][:].rearrange("p w j -> p (w j)"))
-
-        def col_t(u, c):
+        def add_to_columns(u, c):
             g, h = UNITS[u]
             if g == 0:
-                col_b[h, c] = ps.tile([P, J, P], F32, name="cb", tag="cb", bufs=2)
-            for t in range(J):
-                for j in range(J):
-                    nc.tensor.matmul(col_b[h, c][:, t, :], lhsT=dz_t[u][:, j, blk(c, t)], rhs=ident[:], is_transpose=True,
-                                     start=(g == 0 and t == 0 and j == 0), stop=(g == NG - 1 and t == J - 1 and j == J - 1))
+                column_bank[h, c] = psum.tile([P, SLOTS, P], F32, name="column", tag="column", bufs=COLUMN_BANKS)
+            for t in range(SLOTS):
+                for j in range(SLOTS):
+                    nc.tensor.matmul(
+                        column_bank[h, c][:, t, :], lhsT=dz[u][:, j, columns(c, t)], rhs=identity[:], is_transpose=True,
+                        start=(g == 0 and t == 0 and j == 0),
+                        stop=(g == ROW_BLOCKS - 1 and t == SLOTS - 1 and j == SLOTS - 1))
 
-        def col_r(h, c):
-            cc = h * NC + c
-            if h in RSV:
-                for t in range(J):
-                    junk = sb.tile([P, P], BF16, name="junk", tag="junk", bufs=2, align_bytes=64)
-                    nc.scalar.activation(junk[:], col_b[h, c][:, t, :], COPY, scale=-1.0, accum_out=ncol[:, cc, t : t + 1])
+        def finish_columns(h, c):
+            b = h * HALF_BLOCKS + c
+            if h == HALVES - 1:
+                for t in range(SLOTS):
+                    unread = work.tile([P, P], BF16, name="unread", tag="unread", bufs=2, align_bytes=64)
+                    nc.scalar.activation(unread[:], column_bank[h, c][:, t, :], COPY, scale=-1.0,
+                                         accum_out=minus_col[:, b, t : t + 1])
             else:
-                nc.vector.tensor_reduce(ncol[:, cc, :], col_b[h, c][:], AX, ADD, negate=True)
+                nc.vector.tensor_reduce(minus_col[:, b, :], column_bank[h, c][:], AXIS_X, ADD, negate=True)
 
-        def mx0(b, g, j):
-            for cc in range(NCC):
-                q, s = zq[g, cc // NC]
-                a = (cc % NC) * KP + j * P
+        def multiply_0(bank, g, j):
+            for b in range(CENTER_BLOCKS):
+                codes, scales = z_quantized[g, b // HALF_BLOCKS]
+                first = (b % HALF_BLOCKS) * PASS + j * P
                 nc.tensor.matmul_mx(
-                    out=b, lhsT=q[:, a : a + P].bitcast(E5), lhsT_scale=s[:, a : a + P],
-                    rhs=cent_q[:, cc, :].bitcast(E4), rhs_scale=cent_s[:, cc, :],
-                    start=(cc == 0), stop=(cc == NCC - 1))
+                    out=bank,
+                    lhsT=codes[:, first : first + P].bitcast(E5M2X4), lhsT_scale=scales[:, first : first + P],
+                    rhs=centers_codes[:, b, :].bitcast(E4M3X4), rhs_scale=centers_scales[:, b, :],
+                    start=(b == 0), stop=(b == CENTER_BLOCKS - 1))
 
-        def mx1(b, h, c, t):
-            for g in range(NG):
-                q, s = xq[g, h]
+        def multiply_1(bank, h, c, t):
+            for g in range(ROW_BLOCKS):
+                codes, scales = x_quantized[g, h]
                 nc.tensor.matmul_mx(
-                    out=b, lhsT=q[:, blk(c, t)].bitcast(E5), lhsT_scale=s[:, blk(c, t)],
-                    rhs=data_q[:, g, :].bitcast(E4), rhs_scale=data_s[:, g, :],
-                    start=(g == 0), stop=(g == NG - 1))
+                    out=bank,
+                    lhsT=codes[:, columns(c, t)].bitcast(E5M2X4), lhsT_scale=scales[:, columns(c, t)],
+                    rhs=data_codes[:, g, :].bitcast(E4M3X4), rhs_scale=data_scales[:, g, :],
+                    start=(g == 0), stop=(g == ROW_BLOCKS - 1))
 
-        def out_tile(key, i):
-            if i % 2 == 0:
-                ost[key] = sb.tile([P, 2, D], F32, name="o", tag="o", bufs=6, align_bytes=64)
-            return ost[key]
+        def result_pair(key, slot):
+            if slot % 2 == 0:
+                result[key] = work.tile([P, 2, D], F32, name="result", tag="stage", bufs=STAGE_BUFS, align_bytes=64)
+            return result[key]
 
-        def store(dst, row, i, o):
-            nc.sync.dma_start(out=dst[row * KP : (row + 1) * KP, :].rearrange("(p j) w -> p j w", j=J)[:, i - 1 : i + 1, :], in_=o[:])
+        def store(dst, b, slots, tile):
+            rows = dst[b * PASS : (b + 1) * PASS, :].rearrange("(p j) w -> p j w", j=SLOTS)
+            nc.sync.dma_start(out=rows[:, slots, :], in_=tile)
 
-        def epi0(b, g, j):
-            o = out_tile((0, g, j // 2), j)
-            nc.vector.scalar_tensor_tensor(out=o[:, j % 2, :], in0=data_sb[:, g, j, :], scalar=nrow[:, g, j : j + 1],
-                                           in1=b, op0=MULT, op1=ADD)
+        def finish_0(bank, g, j):
+            pair = result_pair((0, g, j // 2), j)
+            nc.vector.scalar_tensor_tensor(out=pair[:, j % 2, :], in0=data_sb[:, g, j, :], scalar=minus_row[:, g, j : j + 1],
+                                           in1=bank, op0=MULT, op1=ADD)
             if j % 2 == 1:
-                later.append((g, j, o))
+                half_done.append((g, slice(j - 1, j + 1), pair))
 
-        def epi0b(g, j, o):
-            nc.vector.tensor_tensor(out=o[:], in0=o[:], in1=gd_t[g][:, j - 1 : j + 1, :], op=ADD)
-            store(out_0, g, j, o)
+        def add_g_data(g, slots, pair):
+            nc.vector.tensor_tensor(out=pair[:], in0=pair[:], in1=g_data[g][:, slots, :], op=ADD)
+            store(out_0, g, slots, pair[:])
 
-        def epi1(b, h, c, t):
-            cc = h * NC + c
-            o = out_tile((1, cc, t // 2), t)
-            nc.vector.scalar_tensor_tensor(out=o[:, t % 2, :], in0=cent_sb[:, cc, t, :], scalar=ncol[:, cc, t : t + 1],
-                                           in1=b, op0=MULT, op1=ADD)
-            if t % 2 == 1:
-                store(out_1, cc, t, o)
+        def finish_1(bank, h, c, t):
+            b = h * HALF_BLOCKS + c
+            pair = result_pair((1, b, t // 2), t)
+            nc.vector.scalar_tensor_tensor(out=pair[:, t % 2, :], in0=centers_sb[:, b, t, :], scalar=minus_col[:, b, t : t + 1],
+                                           in1=bank, op0=MULT, op1=ADD)
+            if b == CENTER_BLOCKS - 1 and t >= SLOTS - 2:
+                store(out_1, b, t, pair[:, t % 2, :])
+            elif t % 2 == 1:
+                store(out_1, b, slice(t - 1, t + 1), pair[:])
 
-        todo, popped, later = [], [], []
+        def start_products(count):
+            for multiply, finish, args in waiting[:count]:
+                for ahead, unused, ahead_args in waiting[:2]:
+                    if ahead is multiply_0 and ahead_args[0] not in g_data:
+                        load_g_data(ahead_args[0])
+                waiting.pop(0)
+                bank = psum.tile([P, D], F32, name="product", tag="product", bufs=PRODUCT_BANKS)
+                multiply(bank[:], *args)
+                started.append((finish, bank, args))
 
-        def pop_jobs(n):
-            for i in range(n):
-                if todo:
-                    mxf, epf, args = todo.pop(0)
-                    if mxf is mx0 and args[1] == 0:
-                        load_gd(args[0])
-                    b = ps.tile([P, D], F32, name="mb", tag="mb", bufs=4)
-                    mxf(b[:], *args)
-                    popped.append((epf, b, args))
+        def finish_products():
+            pairs = list(half_done)
+            half_done.clear()
+            for finish, bank, args in started:
+                finish(bank[:], *args)
+            started.clear()
+            for pair_args in pairs:
+                add_g_data(*pair_args)
 
-        def do_epis():
-            late = list(later)
-            later.clear()
-            for epf, b, args in popped:
-                epf(b[:], *args)
-            popped.clear()
-            for a in late:
-                epi0b(*a)
-
-        C_AT = (6, 8, 10, 12)
-        D_V = (0, 1, 2, 3)
         with tc.manual_schedule():
-            load_dc(data_sb, data, 0)
-            load(0)
-            load_dc(data_sb, data, 1)
-            load(1)
-            load_dc(data_sb, data, 2)
-            load(2)
-            load(3)
-            load_dc(data_sb, data, 3)
-            for n in range(4, 4):
-                load(n)
-            dc_copy("d", data_sb, 0, 0)
-            for u in range(NU + 1):
-                for j in range(J):
-                    n = J * u + j
-                    if u < NU:
-                        stt(u, j)
-                        load(n + 4)
-                    do_epis()
-                    pop_jobs(2 if len(todo) > 3 else 1)
-                    if n in C_AT:
-                        load_dc(cent_sb, centers, C_AT.index(n))
-                    if u >= 1 and j in (0, 2):
-                        col_t(u - 1, (0, 2).index(j))
-                    if u >= 1:
-                        xpiece(u - 1, j)
-                    if u < NU:
-                        transp(u, j)
-                    if u >= 1 and j == 2:
-                        qz(u - 1)
-                    if u >= 1 and j == 3 and UNITS[u - 1][0] == NG - 1:
-                        for c in range(NC):
-                            col_r(UNITS[u - 1][1], c)
-                    if u >= 1 and j == 3:
-                        qx(u - 1, 0)
-                        if u == NU:
-                            qx(u - 1, 1)
-                    if u >= 2 and j == 0:
-                        qx(u - 2, 1)
+            load_block(data_sb, data, 0)
+            load_block(data_sb, data, 1)
+            load_step(0)
+            load_step(1)
+            load_block(data_sb, data, 2)
+            load_step(2)
+            load_block(data_sb, data, 3)
+            load_step(3)
+            interleave_block(0 in VECTOR_DATA, "data", data_sb, 0)
+
+            for u in range(len(UNITS) + 1):
+                for j in range(SLOTS):
+                    step = SLOTS * u + j
+                    if u < len(UNITS):
+                        compute_dz(u, j)
+                        load_step(step + LOAD_AHEAD)
+                    finish_products()
+                    start_products(2 if len(waiting) > BACKLOG else 1)
+                    if step in CENTER_STEPS:
+                        load_block(centers_sb, centers, CENTER_STEPS.index(step))
+                    if u >= 1 and j % 2 == 0:
+                        add_to_columns(u - 1, j // 2)
+                    copy_out_transposed()
+                    if u >= 1 and u - 1 != FIRST_HALF_END:
+                        interleave_piece(u - 1, j)
+                    if u - 1 == FIRST_HALF_END and j < 2:
+                        interleave_piece(u - 1, j)
+                        interleave_piece(u - 1, j + 2)
+                    if u < len(UNITS):
+                        transpose_dz(u, j)
+                    if u >= 1 and j == 1:
+                        quantize_by_centers(u - 1)
+                    if u >= 1 and j == 3 and UNITS[u - 1][0] == ROW_BLOCKS - 1:
+                        for c in range(HALF_BLOCKS):
+                            finish_columns(UNITS[u - 1][1], c)
+                    if u >= 1 and j == 3 and u - 1 != FIRST_HALF_END:
+                        quantize_by_tokens(u - 1, 0)
+                        if u == len(UNITS):
+                            quantize_by_tokens(u - 1, 1)
+                    if u >= 2 and j == 0 and u - 2 != FIRST_HALF_END:
+                        quantize_by_tokens(u - 2, 1)
+                    if u - 1 == FIRST_HALF_END and j == 2:
+                        quantize_by_tokens(u - 1, 0)
+                        quantize_by_tokens(u - 1, 1)
                     if u == 0:
-                        if j < 3:
-                            dc_copy("d", data_sb, j + 1, 0 if j + 1 in D_V else 1)
-                        dc_quant("d", data_q, data_s, j)
-                    if n - 4 in C_AT:
-                        dc_copy("c", cent_sb, C_AT.index(n - 4), 1)
-                    if n - 6 in C_AT:
-                        dc_quant("c", cent_q, cent_s, C_AT.index(n - 6))
-                    pass
-            while todo or popped or later:
-                do_epis()
-                pop_jobs(2)
+                        if j + 1 < ROW_BLOCKS:
+                            interleave_block(j + 1 in VECTOR_DATA, "data", data_sb, j + 1)
+                        quantize_block("data", data_codes, data_scales, j)
+                    if step - COPY_DELAY in CENTER_STEPS:
+                        interleave_block(False, "centers", centers_sb, CENTER_STEPS.index(step - COPY_DELAY))
+                    if step - QUANTIZE_DELAY in CENTER_STEPS:
+                        quantize_block("centers", centers_codes, centers_scales, CENTER_STEPS.index(step - QUANTIZE_DELAY))
+            while waiting or started or half_done:
+                finish_products()
+                start_products(2)

from contextlib import ExitStack

import concourse.mybir as mybir
from concourse.masks import make_identity

N, D, K = 2048, 512, 2048
FLOPS = 2 * 2 * N * K * D

F32 = mybir.dt.float32
BF16 = mybir.dt.bfloat16
U32 = mybir.dt.uint32
U8 = mybir.dt.uint8
E4M3X4 = mybir.dt.float8_e4m3fn_x4
E5M2X4 = mybir.dt.float8_e5m2_x4
COPY = mybir.ActivationFunctionType.Copy
MULT = mybir.AluOpType.mult
ADD = mybir.AluOpType.add
SUB = mybir.AluOpType.subtract
AXIS_X = mybir.AxisListType.X

P = 128
SLOTS = 4
PASS = P * SLOTS
ROW_BLOCKS = N // PASS
CENTER_BLOCKS = K // PASS
HALF_BLOCKS = 2
HALF = HALF_BLOCKS * PASS
HALVES = K // HALF
PIECE = HALF // SLOTS

UNITS = [(g, h) for h in range(HALVES) for g in range(ROW_BLOCKS)]
FIRST_HALF_END = ROW_BLOCKS - 1

VECTOR_PIECES = [(0, 3), (1, 0), (1, 2), (2, 3), (3, 0), (3, 2)]
VECTOR_DATA = (0, 2)

CENTER_STEPS = (12, 14, 16, 17)
COPY_DELAY = 4
QUANTIZE_DELAY = 6

LOAD_AHEAD = 4
BACKLOG = 6

GRAD_BUFS, RBF_BUFS, DZ_BUFS = 3, 4, 3
Z_BUFS, X_BUFS, Z_CODE_BUFS, X_CODE_BUFS = 2, 3, 6, 5
STAGE_BUFS = 6
TRANSPOSE_BANKS, COLUMN_BANKS, PRODUCT_BANKS = 3, 2, 3


def tile_dicgaussianrbf_v_kernel(tc, data, centers, rbfs, grad_out, out_0, out_1):
    nc = tc.nc
    with ExitStack() as ctx:
        keep = ctx.enter_context(tc.tile_pool(name="keep", bufs=1))
        work = ctx.enter_context(tc.tile_pool(name="work", bufs=1))
        psum = ctx.enter_context(tc.psum_pool(name="psum", bufs=1))

        identity = keep.tile([P, P], F32, name="identity")
        make_identity(nc, identity[:])
        first_copy = keep.tile([P, 1], F32, name="first_copy")
        nc.scalar.copy(first_copy[:], identity[:, 0:1])

        data_sb = keep.tile([P, ROW_BLOCKS, SLOTS, D], BF16, name="data_sb", align_bytes=64)
        centers_sb = keep.tile([P, CENTER_BLOCKS, SLOTS, D], BF16, name="centers_sb", align_bytes=64)
        data_codes = keep.tile([P, ROW_BLOCKS, D], U32, name="data_codes", align_bytes=64)
        data_scales = keep.tile([P, ROW_BLOCKS, D], U8, name="data_scales", align_bytes=64)
        centers_codes = keep.tile([P, CENTER_BLOCKS, D], U32, name="centers_codes", align_bytes=64)
        centers_scales = keep.tile([P, CENTER_BLOCKS, D], U8, name="centers_scales", align_bytes=64)
        row_parts = keep.tile([P, ROW_BLOCKS, HALVES, SLOTS], F32, name="row_parts")
        minus_row = keep.tile([P, ROW_BLOCKS, SLOTS], F32, name="minus_row")
        minus_col = keep.tile([P, CENTER_BLOCKS, SLOTS], F32, name="minus_col")

        grad, rbf, dz, x, z, z_quantized, x_quantized = {}, {}, {}, {}, {}, {}, {}
        g_data, column_bank, grouped, result = {}, {}, {}, {}
        full_banks = []
        waiting = []
        started = []
        half_done = []

        def load_step(step):
            u, j = step // SLOTS, step % SLOTS
            if u == len(UNITS):
                return
            g, h = UNITS[u]
            rows = slice(g * PASS, (g + 1) * PASS)
            grad_cols = slice(1 + D + h * HALF, 1 + D + (h + 1) * HALF)
            grad_rows = grad_out[rows, grad_cols].rearrange("(p j) w -> p j w", j=SLOTS)
            rbf_rows = rbfs[rows, h * HALF : (h + 1) * HALF].rearrange("(p j) w -> p j w", j=SLOTS)
            if j % 2 == 0:
                grad[u, j // 2] = work.tile([P, 2, HALF], BF16, name="grad", tag="grad", bufs=GRAD_BUFS, align_bytes=64)
            if step < 2:
                nc.sync.dma_start(out=grad[u, 0][:, j, :], in_=grad_rows[:, j, :])
            elif j % 2 == 0:
                nc.sync.dma_start(out=grad[u, j // 2][:], in_=grad_rows[:, j : j + 2, :])
            rbf[u, j] = work.tile([P, HALF], F32, name="rbf", tag="rbf", bufs=RBF_BUFS, align_bytes=64)
            nc.sync.dma_start(out=rbf[u, j][:], in_=rbf_rows[:, j, :])

        def load_block(dst, src, b):
            rows = src[b * PASS : (b + 1) * PASS, :]
            nc.sync.dma_start(out=dst[:, b, :, :], in_=rows.rearrange("(p j) w -> p j w", j=SLOTS))

        def load_g_data(g):
            g_data[g] = work.tile([P, SLOTS, D], BF16, name="g_data", tag="stage", bufs=STAGE_BUFS, align_bytes=64)
            rows = grad_out[g * PASS : (g + 1) * PASS, 1 : 1 + D]
            nc.sync.dma_start(out=g_data[g][:], in_=rows.rearrange("(p j) w -> p j w", j=SLOTS))

        def compute_dz(u, j):
            g, h = UNITS[u]
            if j == 0:
                dz[u] = work.tile([P, SLOTS, HALF], F32, name="dz", tag="dz", bufs=DZ_BUFS, align_bytes=64)
            nc.vector.scalar_tensor_tensor(
                out=dz[u][:, j, :].rearrange("p (t q) -> p q t", t=SLOTS),
                in0=grad[u, j // 2][:, j % 2, :].rearrange("p (q t) -> p q t", t=SLOTS),
                scalar=10.0,
                in1=rbf[u, j][:].rearrange("p (q t) -> p q t", t=SLOTS),
                op0=MULT, op1=MULT, accum_out=row_parts[:, g, h, j : j + 1])

        def columns(c, t):
            first = (t * HALF_BLOCKS + c) * P
            return slice(first, first + P)

        def transpose_dz(u, j):
            for c in range(HALF_BLOCKS):
                bank = psum.tile([P, SLOTS, P], F32, name="transposed", tag="transposed", bufs=TRANSPOSE_BANKS)
                for t in range(SLOTS):
                    nc.tensor.transpose(bank[:, t, :], dz[u][:, j, columns(c, t)], identity[:])
                full_banks.append((u, c, j, bank))

        def copy_out_transposed():
            while full_banks:
                u, c, j, bank = full_banks.pop(0)
                if u not in z:
                    z[u] = work.tile([P, HALF_BLOCKS, SLOTS, P, SLOTS], BF16, name="z", tag="z", bufs=Z_BUFS, align_bytes=64)
                nc.scalar.copy(z[u][:, c, j, :, :].rearrange("p (r i) t -> p r t i", i=4),
                               bank[:].rearrange("p t (r i) -> p r t i", i=4))

        def interleave(on_vector, out, in_):
            out = out.rearrange("p (c i) j -> p c j i", i=4)
            in_ = in_.rearrange("p j (c i) -> p c j i", i=4)
            if on_vector:
                nc.vector.tensor_copy(out, in_)
            else:
                nc.scalar.copy(out, in_)

        def interleave_piece(u, k):
            if k % 2 == 0:
                x[u, k // 2] = work.tile([P, 2 * PIECE, SLOTS], BF16, name="x", tag="x", bufs=X_BUFS, align_bytes=64)
            first = (k % 2) * PIECE
            interleave((u, k) in VECTOR_PIECES, x[u, k // 2][:, first : first + PIECE, :],
                       dz[u][:, :, k * PIECE : (k + 1) * PIECE])

        def interleave_block(on_vector, name, src, b):
            grouped[name, b] = work.tile([P, D, SLOTS], BF16, name="grouped", tag="stage", bufs=STAGE_BUFS, align_bytes=64)
            interleave(on_vector, grouped[name, b][:], src[:, b, :, :])

        def quantize_block(name, codes, scales, b):
            nc.vector.quantize_mx(out=codes[:, b, :].bitcast(E4M3X4), scales=scales[:, b, :],
                                  in_=grouped[name, b][:].rearrange("p w j -> p (w j)"))

        def quantize_by_centers(u):
            g, h = UNITS[u]
            codes = work.tile([P, HALF], U32, name="z_codes", tag="z_codes", bufs=Z_CODE_BUFS, align_bytes=64)
            scales = work.tile([P, HALF], U8, name="z_scales", tag="z_scales", bufs=Z_CODE_BUFS, align_bytes=64)
            nc.vector.quantize_mx(out=codes[:].bitcast(E5M2X4), scales=scales[:],
                                  in_=z[u][:].rearrange("p c j r t -> p (c j r t)"))
            z_quantized[g, h] = (codes, scales)
            if h == HALVES - 1:
                nc.vector.scalar_tensor_tensor(out=minus_row[:, g, :], in0=row_parts[:, g, 0, :], scalar=-1.0,
                                               in1=row_parts[:, g, 1, :], op0=MULT, op1=SUB)
                for j in range(SLOTS):
                    waiting.append((multiply_0, finish_0, (g, j)))

        def quantize_by_tokens(u, part):
            g, h = UNITS[u]
            if part == 0:
                codes = work.tile([P, HALF], U32, name="x_codes", tag="x_codes", bufs=X_CODE_BUFS, align_bytes=64)
                scales = work.tile([P, HALF], U8, name="x_scales", tag="x_scales", bufs=X_CODE_BUFS, align_bytes=64)
                x_quantized[g, h] = (codes, scales)
            codes, scales = x_quantized[g, h]
            cols = slice(part * HALF // 2, (part + 1) * HALF // 2)
            nc.vector.quantize_mx(out=codes[:, cols].bitcast(E5M2X4), scales=scales[:, cols],
                                  in_=x[u, part][:].rearrange("p w j -> p (w j)"))
            if part == 1 and g == ROW_BLOCKS - 1:
                for c in range(HALF_BLOCKS):
                    for t in range(SLOTS):
                        waiting.append((multiply_1, finish_1, (h, c, t)))

        def add_to_columns(u, c):
            g, h = UNITS[u]
            if g == 0:
                column_bank[h, c] = psum.tile([P, SLOTS, P], F32, name="column", tag="column", bufs=COLUMN_BANKS)
            for t in range(SLOTS):
                for j in range(SLOTS):
                    nc.tensor.matmul(
                        column_bank[h, c][:, t, :], lhsT=dz[u][:, j, columns(c, t)], rhs=identity[:], is_transpose=True,
                        start=(g == 0 and t == 0 and j == 0),
                        stop=(g == ROW_BLOCKS - 1 and t == SLOTS - 1 and j == SLOTS - 1))

        def finish_columns(h, c):
            b = h * HALF_BLOCKS + c
            if h == HALVES - 1:
                for t in range(SLOTS):
                    unread = work.tile([P, P], BF16, name="unread", tag="unread", bufs=2, align_bytes=64)
                    nc.scalar.activation(unread[:], column_bank[h, c][:, t, :], COPY, scale=-1.0,
                                         accum_out=minus_col[:, b, t : t + 1])
            else:
                nc.vector.tensor_reduce(minus_col[:, b, :], column_bank[h, c][:], AXIS_X, ADD, negate=True)

        def multiply_0(bank, g, j):
            for b in range(CENTER_BLOCKS):
                codes, scales = z_quantized[g, b // HALF_BLOCKS]
                first = (b % HALF_BLOCKS) * PASS + j * P
                nc.tensor.matmul_mx(
                    out=bank,
                    lhsT=codes[:, first : first + P].bitcast(E5M2X4), lhsT_scale=scales[:, first : first + P],
                    rhs=centers_codes[:, b, :].bitcast(E4M3X4), rhs_scale=centers_scales[:, b, :],
                    start=(b == 0), stop=(b == CENTER_BLOCKS - 1))

        def multiply_1(bank, h, c, t):
            for g in range(ROW_BLOCKS):
                codes, scales = x_quantized[g, h]
                nc.tensor.matmul_mx(
                    out=bank,
                    lhsT=codes[:, columns(c, t)].bitcast(E5M2X4), lhsT_scale=scales[:, columns(c, t)],
                    rhs=data_codes[:, g, :].bitcast(E4M3X4), rhs_scale=data_scales[:, g, :],
                    start=(g == 0), stop=(g == ROW_BLOCKS - 1))

        def result_pair(key, slot):
            if slot % 2 == 0:
                result[key] = work.tile([P, 2, D], F32, name="result", tag="stage", bufs=STAGE_BUFS, align_bytes=64)
            return result[key]

        def store(dst, b, slots, tile):
            rows = dst[b * PASS : (b + 1) * PASS, :].rearrange("(p j) w -> p j w", j=SLOTS)
            nc.sync.dma_start(out=rows[:, slots, :], in_=tile)

        def finish_0(bank, g, j):
            pair = result_pair((0, g, j // 2), j)
            nc.vector.scalar_tensor_tensor(out=pair[:, j % 2, :], in0=data_sb[:, g, j, :], scalar=minus_row[:, g, j : j + 1],
                                           in1=bank, op0=MULT, op1=ADD)
            if j % 2 == 1:
                half_done.append((g, slice(j - 1, j + 1), pair))

        def add_g_data(g, slots, pair):
            nc.vector.tensor_tensor(out=pair[:], in0=pair[:], in1=g_data[g][:, slots, :], op=ADD)
            store(out_0, g, slots, pair[:])

        def finish_1(bank, h, c, t):
            b = h * HALF_BLOCKS + c
            pair = result_pair((1, b, t // 2), t)
            nc.vector.scalar_tensor_tensor(out=pair[:, t % 2, :], in0=centers_sb[:, b, t, :], scalar=minus_col[:, b, t : t + 1],
                                           in1=bank, op0=MULT, op1=ADD)
            if b == CENTER_BLOCKS - 1 and t >= SLOTS - 2:
                store(out_1, b, t, pair[:, t % 2, :])
            elif t % 2 == 1:
                store(out_1, b, slice(t - 1, t + 1), pair[:])

        def start_products(count):
            for multiply, finish, args in waiting[:count]:
                for ahead, unused, ahead_args in waiting[:2]:
                    if ahead is multiply_0 and ahead_args[0] not in g_data:
                        load_g_data(ahead_args[0])
                waiting.pop(0)
                bank = psum.tile([P, D], F32, name="product", tag="product", bufs=PRODUCT_BANKS)
                multiply(bank[:], *args)
                started.append((finish, bank, args))

        def finish_products():
            pairs = list(half_done)
            half_done.clear()
            for finish, bank, args in started:
                finish(bank[:], *args)
            started.clear()
            for pair_args in pairs:
                add_g_data(*pair_args)

        with tc.manual_schedule():
            load_block(data_sb, data, 0)
            load_block(data_sb, data, 1)
            load_step(0)
            load_step(1)
            load_block(data_sb, data, 2)
            load_step(2)
            load_block(data_sb, data, 3)
            load_step(3)
            interleave_block(0 in VECTOR_DATA, "data", data_sb, 0)

            for u in range(len(UNITS) + 1):
                for j in range(SLOTS):
                    step = SLOTS * u + j
                    if u < len(UNITS):
                        compute_dz(u, j)
                        load_step(step + LOAD_AHEAD)
                    finish_products()
                    start_products(2 if len(waiting) > BACKLOG else 1)
                    if step in CENTER_STEPS:
                        load_block(centers_sb, centers, CENTER_STEPS.index(step))
                    if u >= 1 and j % 2 == 0:
                        add_to_columns(u - 1, j // 2)
                    copy_out_transposed()
                    if u >= 1 and u - 1 != FIRST_HALF_END:
                        interleave_piece(u - 1, j)
                    if u - 1 == FIRST_HALF_END and j < 2:
                        interleave_piece(u - 1, j)
                        interleave_piece(u - 1, j + 2)
                    if u < len(UNITS):
                        transpose_dz(u, j)
                    if u >= 1 and j == 1:
                        quantize_by_centers(u - 1)
                    if u >= 1 and j == 3 and UNITS[u - 1][0] == ROW_BLOCKS - 1:
                        for c in range(HALF_BLOCKS):
                            finish_columns(UNITS[u - 1][1], c)
                    if u >= 1 and j == 3 and u - 1 != FIRST_HALF_END:
                        quantize_by_tokens(u - 1, 0)
                        if u == len(UNITS):
                            quantize_by_tokens(u - 1, 1)
                    if u >= 2 and j == 0 and u - 2 != FIRST_HALF_END:
                        quantize_by_tokens(u - 2, 1)
                    if u - 1 == FIRST_HALF_END and j == 2:
                        quantize_by_tokens(u - 1, 0)
                        quantize_by_tokens(u - 1, 1)
                    if u == 0:
                        if j + 1 < ROW_BLOCKS:
                            interleave_block(j + 1 in VECTOR_DATA, "data", data_sb, j + 1)
                        quantize_block("data", data_codes, data_scales, j)
                    if step - COPY_DELAY in CENTER_STEPS:
                        interleave_block(False, "centers", centers_sb, CENTER_STEPS.index(step - COPY_DELAY))
                    if step - QUANTIZE_DELAY in CENTER_STEPS:
                        quantize_block("centers", centers_codes, centers_scales, CENTER_STEPS.index(step - QUANTIZE_DELAY))
            while waiting or started or half_done:
                finish_products()
                start_products(2)
